import numpy as np
import ml_dtypes


def mxq(x, axis, fmt="e4m3"):
    dtype, down = {"e4m3": (ml_dtypes.float8_e4m3fn, 7), "e5m2": (ml_dtypes.float8_e5m2, 14)}[fmt]
    v = np.moveaxis(np.asarray(x, np.float32).astype(ml_dtypes.bfloat16).astype(np.float64), axis, -1)
    blocks = v.reshape(v.shape[:-1] + (-1, 32))
    amax = np.abs(blocks).max(-1, keepdims=True)
    byte = np.maximum(np.where(amax > 0, np.frexp(amax)[1] - 1 + 127, 0) - down, 1)
    scale = np.exp2(byte - 127.0)
    codes = (blocks / scale).astype(np.float32).astype(dtype).astype(np.float64)
    return np.moveaxis((codes * scale).reshape(v.shape), -1, axis)


WIDE = False


def mx_kscale(k):
    if not WIDE:
        return np.ones(k)
    levels = np.array([10, -10, 5, -5, 0])
    a = np.random.permutation(np.resize(levels, k // 512 * 4)).reshape(k // 512, 4)
    idx = np.arange(k)
    return np.exp2(a[idx // 512, idx % 128 // 32])


BF16 = ml_dtypes.bfloat16


def bf(x):
    return np.asarray(x, np.float32).astype(BF16)


def f64(x):
    return np.asarray(x).astype(np.float64)


E2M1 = np.array([0.0, 0.5, 1.0, 1.5, 2.0, 3.0, 4.0, 6.0, -0.0, -0.5, -1.0, -1.5, -2.0, -3.0, -4.0, -6.0])


def pack_weight(w, fmt):
    k, n = w.shape
    w = f64(bf(w)).reshape(k // 32, 32, n)
    amax = np.abs(w).max(1)
    if fmt == "e4m3":
        byte = np.frexp(amax)[1] - 1 + 127 - 7
    else:
        mant, ex = np.frexp(amax / 6.0)
        byte = np.where(mant > 0.5, ex, ex - 1) + 127
    byte = np.clip(np.where(amax > 0, byte, 1), 1, 254)
    scaled = (w * np.exp2(127.0 - byte)[:, None, :]).reshape(k, n).astype(np.float32)
    by_word = np.ascontiguousarray(scaled.reshape(k // 512, 128, 4, n).transpose(0, 1, 3, 2))
    if fmt == "e4m3":
        words = by_word.astype(ml_dtypes.float8_e4m3fn).view(np.uint8)
    else:
        c = by_word.astype(ml_dtypes.float4_e2m1fn).view(np.uint8) & 0xF
        words = c[..., 0::2] | (c[..., 1::2] << 4)
    return np.ascontiguousarray(words), np.ascontiguousarray(byte.astype(np.uint8).reshape(k // 512, 16, n))


def unpack_weight(words, scales, fmt):
    g, p, n, _ = words.shape
    if fmt == "e4m3":
        vals = np.ascontiguousarray(words).view(ml_dtypes.float8_e4m3fn).astype(np.float64)
    else:
        nib = np.empty((g, p, n, 4), np.uint8)
        nib[..., 0::2] = words & 0xF
        nib[..., 1::2] = words >> 4
        vals = E2M1[nib]
    vals = vals * np.repeat(np.exp2(scales.astype(np.float64) - 127.0), 8, axis=1)[..., None]
    return vals.transpose(0, 1, 3, 2).reshape(g * 512, n)

def pack4(w):
    words, scales = pack_weight(w, "e2m1")
    return words.reshape(words.shape[0], 128, -1), scales


def unpack4(words, scales):
    return unpack_weight(words.reshape(words.shape[0], 128, -1, 2), scales, "e2m1")


B, CB, CD, H, W = 4, 2, 512, 32, 32
C = CB * CD


def erf(z):
    z = np.clip(z, -6.0, 6.0)
    z2 = 2.0 * z * z
    term = z.copy()
    tot = z.copy()
    for n in range(1, 101):
        term *= z2
        term /= 2 * n + 1
        tot += term
    return 2.0 / np.sqrt(np.pi) * np.exp(-z * z) * tot


def gelu_erf(v):
    return 0.5 * v * (1.0 + erf(v / np.sqrt(2.0)))


def setup_inputs():
    s = mx_kscale(CD)
    s = s / s.max()
    sc = np.tile(s, CB)
    x = bf(np.random.standard_normal((B, C, H, W)) * sc[None, :, None, None])
    stack = np.random.standard_normal((CB, CD, CD)) / np.sqrt(CD) / s[None, :, None]
    words, scales = pack4(stack.reshape(-1, CD))
    return {"x": x, "wc_words": words, "wc_scales": scales}


def reference(x, wc_words, wc_scales):
    x = f64(x)
    xr = np.transpose(x, (0, 2, 3, 1)).reshape(B, H, W, CB, CD)
    xb = xr.transpose(3, 0, 1, 2, 4).reshape(CB, B * H * W, CD)
    out = mxq(xb, 2, "e4m3") @ unpack4(wc_words, wc_scales).reshape(CB, CD, CD)
    out = out.reshape(CB, B, H, W, CD).transpose(1, 2, 3, 0, 4)
    out = out.reshape(B, H, W, C).transpose(0, 3, 1, 2)
    return gelu_erf(x + out)

@@ -1,0 +1,128 @@
+import concourse.mybir as mybir
+
+BF16 = mybir.dt.bfloat16
+F32 = mybir.dt.float32
+I32 = mybir.dt.int32
+U8 = mybir.dt.uint8
+U32 = mybir.dt.uint32
+FP8X4 = mybir.dt.float8_e4m3fn_x4
+FP4X4 = mybir.dt.float4_e2m1fn_x4
+
+P = 128
+PACK = 4
+BATCH = 4
+BLOCKS = 2
+CD = P * PACK
+PIXELS = 32 * 32
+UNITS = BATCH * BLOCKS
+M_TILES = CD // P
+N_TILE = 512
+HALVES = PIXELS // N_TILE
+M_PAIR = 2
+
+FLOPS = 2 * BATCH * PIXELS * BLOCKS * CD * CD
+
+
+def tile_spectralchannelmixing_t_e_kernel(tc, x, wc_words, wc_scales, out):
+    nc = tc.nc
+    x_rows = x.rearrange("b c h w -> b c (h w)")
+    out_rows = out.rearrange("b c h w -> b c (h w)")
+
+    with (
+        tc.tile_pool(name="consts", bufs=1) as consts,
+        tc.tile_pool(name="inputs", bufs=UNITS) as inputs,
+        tc.tile_pool(name="quant", bufs=2) as quant,
+        tc.tile_pool(name="results", bufs=6) as results,
+        tc.psum_pool(name="psum", bufs=8) as psum,
+    ):
+        warm = consts.tile([P, 1], F32)
+        nc.vector.memset(warm[:], 0.0)
+        nc.scalar.activation(out=warm[:], in_=warm[:], func=mybir.ActivationFunctionType.Gelu)
+
+        w_scales = consts.tile([P, BLOCKS, CD], U8, align_bytes=64)
+        nc.vector.memset(w_scales[:].bitcast(I32), 0)
+        w_words = consts.tile([P, BLOCKS, 2 * CD], U8, align_bytes=64)
+
+        packed = []
+        resid = []
+        for u in range(UNITS):
+            b, i = divmod(u, BLOCKS)
+            unit_rows = x_rows[b, i * CD : (i + 1) * CD, :]
+            packed_u = inputs.tile([P, PACK, PIXELS], BF16, name="packed")
+            nc.sync.dma_start(out=packed_u[:], in_=unit_rows.rearrange("(p t) s -> p t s", t=PACK))
+            if u == 0:
+                nc.sync.dma_start(
+                    out=w_words[:].bitcast(I32),
+                    in_=wc_words.rearrange("g p n -> p g n").bitcast(I32),
+                )
+                for quad in range(4):
+                    nc.sync.dma_start(
+                        out=w_scales[32 * quad : 32 * quad + 4, :, :].bitcast(I32),
+                        in_=wc_scales[:, 4 * quad : 4 * quad + 4, :]
+                        .rearrange("g r n -> r g n")
+                        .bitcast(I32),
+                    )
+            resid_u = inputs.tile([P, M_TILES, PIXELS], BF16, name="resid")
+            nc.sync.dma_start(out=resid_u[:], in_=unit_rows.rearrange("(m q) s -> q m s", q=P))
+            packed.append(packed_u)
+            resid.append(resid_u)
+
+        def regroup(u):
+            grouped = quant.tile([P, PIXELS, PACK], BF16, align_bytes=64, name="grouped")
+            nc.vector.tensor_copy(
+                out=grouped[:, :N_TILE, :].rearrange("p (c r) t -> p c t r", r=4),
+                in_=packed[u][:, :, :N_TILE].rearrange("p t (c r) -> p c t r", r=4),
+            )
+            nc.scalar.copy(
+                out=grouped[:, N_TILE:, :].rearrange("p (c r) t -> p c t r", r=4),
+                in_=packed[u][:, :, N_TILE:].rearrange("p t (c r) -> p c t r", r=4),
+            )
+            return grouped
+
+        def mix(u, grouped):
+            b, i = divmod(u, BLOCKS)
+            x_codes = quant.tile([P, PIXELS], U32, align_bytes=64, name="x_codes")
+            x_scales = quant.tile([P, PIXELS], U8, align_bytes=64, name="x_scales")
+            for half in range(HALVES):
+                s_cols = slice(half * N_TILE, (half + 1) * N_TILE)
+                nc.vector.quantize_mx(
+                    out=x_codes[:, s_cols].bitcast(FP8X4),
+                    scales=x_scales[:, s_cols],
+                    in_=grouped[:, s_cols, :].rearrange("p s t -> p (s t)"),
+                )
+            unit_out = out_rows[b, i * CD : (i + 1) * CD, :].rearrange("(m q) s -> q m s", q=P)
+            for m0 in range(0, M_TILES, M_PAIR):
+                result = results.tile([P, M_PAIR, PIXELS], F32, name="result")
+                for k in range(M_PAIR):
+                    m = m0 + k
+                    for half in range(HALVES):
+                        s_cols = slice(half * N_TILE, (half + 1) * N_TILE)
+                        acc = psum.tile([P, N_TILE], F32, name="acc")
+                        nc.tensor.matmul_mx(
+                            out=acc[:],
+                            lhsT=w_words[:, i, 2 * P * m : 2 * P * (m + 1)].bitcast(FP4X4),
+                            lhsT_scale=w_scales[:, i, P * m : P * (m + 1)],
+                            rhs=x_codes[:, s_cols].bitcast(FP8X4),
+                            rhs_scale=x_scales[:, s_cols],
+                            start=True,
+                            stop=True,
+                        )
+                        nc.vector.tensor_tensor(
+                            out=result[:, k, s_cols],
+                            in0=acc[:],
+                            in1=resid[u][:, m, s_cols],
+                            op=mybir.AluOpType.add,
+                        )
+                    nc.scalar.activation(
+                        out=result[:, k, :],
+                        in_=result[:, k, :],
+                        func=mybir.ActivationFunctionType.Gelu,
+                    )
+                nc.scalar.dma_start(out=unit_out[:, m0 : m0 + M_PAIR, :], in_=result[:])
+
+        grouped_next = regroup(0)
+        for u in range(UNITS):
+            grouped_now = grouped_next
+            if u + 1 < UNITS:
+                grouped_next = regroup(u + 1)
+            mix(u, grouped_now)

@@ -1,4 +1,5 @@
 import concourse.mybir as mybir
+from concourse.masks import make_identity
 
 BF16 = mybir.dt.bfloat16
 F32 = mybir.dt.float32
@@ -19,6 +20,9 @@ M_TILES = CD // P
 N_TILE = 512
 HALVES = PIXELS // N_TILE
 M_PAIR = 2
+LOADED_TILES = 2
+MOVED_TILES = M_TILES - LOADED_TILES
+WORDS = PIXELS // 2
 
 FLOPS = 2 * BATCH * PIXELS * BLOCKS * CD * CD
 
@@ -32,12 +36,17 @@ def tile_spectralchannelmixing_t_e_kernel(tc, x, wc_words, wc_scales, out):
         tc.tile_pool(name="consts", bufs=1) as consts,
         tc.tile_pool(name="inputs", bufs=UNITS) as inputs,
         tc.tile_pool(name="quant", bufs=2) as quant,
+        tc.tile_pool(name="moving", bufs=3) as moving,
         tc.tile_pool(name="results", bufs=6) as results,
-        tc.psum_pool(name="psum", bufs=8) as psum,
+        tc.psum_pool(name="psum_move", bufs=2) as psum_move,
+        tc.psum_pool(name="psum_mix", bufs=4) as psum_mix,
     ):
         warm = consts.tile([P, 1], F32)
         nc.vector.memset(warm[:], 0.0)
         nc.scalar.activation(out=warm[:], in_=warm[:], func=mybir.ActivationFunctionType.Gelu)
+
+        identity = consts.tile([P, P], F32)
+        make_identity(nc, identity[:])
 
         w_scales = consts.tile([P, BLOCKS, CD], U8, align_bytes=64)
         nc.vector.memset(w_scales[:].bitcast(I32), 0)
@@ -63,21 +72,53 @@ def tile_spectralchannelmixing_t_e_kernel(tc, x, wc_words, wc_scales, out):
                         .bitcast(I32),
                     )
             resid_u = inputs.tile([P, M_TILES, PIXELS], BF16, name="resid")
-            nc.sync.dma_start(out=resid_u[:], in_=unit_rows.rearrange("(m q) s -> q m s", q=P))
+            nc.sync.dma_start(
+                out=resid_u[:, :LOADED_TILES, :],
+                in_=unit_rows[: LOADED_TILES * P, :].rearrange("(m q) s -> q m s", q=P),
+            )
             packed.append(packed_u)
             resid.append(resid_u)
 
         def regroup(u):
             grouped = quant.tile([P, PIXELS, PACK], BF16, align_bytes=64, name="grouped")
-            nc.vector.tensor_copy(
-                out=grouped[:, :N_TILE, :].rearrange("p (c r) t -> p c t r", r=4),
-                in_=packed[u][:, :, :N_TILE].rearrange("p t (c r) -> p c t r", r=4),
-            )
-            nc.scalar.copy(
-                out=grouped[:, N_TILE:, :].rearrange("p (c r) t -> p c t r", r=4),
-                in_=packed[u][:, :, N_TILE:].rearrange("p t (c r) -> p c t r", r=4),
-            )
+            for half in range(HALVES):
+                s_cols = slice(half * N_TILE, (half + 1) * N_TILE)
+                nc.gpsimd.tensor_scalar(
+                    out=grouped[:, s_cols, :],
+                    in0=packed[u][:, :, s_cols].rearrange("p t s -> p s t"),
+                    scalar1=1.0,
+                    scalar2=0.0,
+                    op0=mybir.AluOpType.mult,
+                    op1=mybir.AluOpType.add,
+                )
             return grouped
+
+        def move_residual(u):
+            packed_words = packed[u][:].bitcast(F32)
+            resid_words = resid[u][:].bitcast(F32)
+            for w0 in range(0, WORDS, P):
+                by_pixel_ps = psum_move.tile([P, PACK, P], F32, name="by_pixel_ps")
+                for t in range(PACK):
+                    nc.tensor.transpose(
+                        out=by_pixel_ps[:, t, :],
+                        in_=packed_words[:, t, w0 : w0 + P],
+                        identity=identity[:],
+                    )
+                by_pixel = moving.tile([P, MOVED_TILES * P], F32, name="by_pixel")
+                nc.scalar.copy(
+                    out=by_pixel[:].rearrange("v (p t) -> v p t", t=PACK),
+                    in_=by_pixel_ps[:, :, LOADED_TILES * P // PACK :].rearrange("v t p -> v p t"),
+                )
+                by_channel_ps = psum_move.tile([P, MOVED_TILES, P], F32, name="by_channel_ps")
+                for k in range(MOVED_TILES):
+                    nc.tensor.transpose(
+                        out=by_channel_ps[:, k, :],
+                        in_=by_pixel[:, k * P : (k + 1) * P],
+                        identity=identity[:],
+                    )
+                nc.vector.tensor_copy(
+                    out=resid_words[:, LOADED_TILES:, w0 : w0 + P], in_=by_channel_ps[:]
+                )
 
         def mix(u, grouped):
             b, i = divmod(u, BLOCKS)
@@ -97,7 +138,7 @@ def tile_spectralchannelmixing_t_e_kernel(tc, x, wc_words, wc_scales, out):
                     m = m0 + k
                     for half in range(HALVES):
                         s_cols = slice(half * N_TILE, (half + 1) * N_TILE)
-                        acc = psum.tile([P, N_TILE], F32, name="acc")
+                        acc = psum_mix.tile([P, N_TILE], F32, name="acc")
                         nc.tensor.matmul_mx(
                             out=acc[:],
                             lhsT=w_words[:, i, 2 * P * m : 2 * P * (m + 1)].bitcast(FP4X4),
@@ -121,8 +162,10 @@ def tile_spectralchannelmixing_t_e_kernel(tc, x, wc_words, wc_scales, out):
                 nc.scalar.dma_start(out=unit_out[:, m0 : m0 + M_PAIR, :], in_=result[:])
 
         grouped_next = regroup(0)
+        move_residual(0)
         for u in range(UNITS):
             grouped_now = grouped_next
             if u + 1 < UNITS:
                 grouped_next = regroup(u + 1)
+                move_residual(u + 1)
             mix(u, grouped_now)

@@ -19,10 +19,19 @@ UNITS = BATCH * BLOCKS
 M_TILES = CD // P
 N_TILE = 512
 HALVES = PIXELS // N_TILE
-M_PAIR = 2
 LOADED_TILES = 2
 MOVED_TILES = M_TILES - LOADED_TILES
 WORDS = PIXELS // 2
+GROUPS = WORDS // P
+STEPS = UNITS * M_TILES
+PREFETCH = 3
+
+TO_PIXELS_LEAD = 4
+SORT_LEAD = 3
+TO_CHANNELS_LEAD = 2
+KEEP_LEAD = 1
+ADD_LAG = 1
+GELU_LAG = 3
 
 FLOPS = 2 * BATCH * PIXELS * BLOCKS * CD * CD
 
@@ -35,11 +44,13 @@ def tile_spectralchannelmixing_t_e_kernel(tc, x, wc_words, wc_scales, out):
     with (
         tc.tile_pool(name="consts", bufs=1) as consts,
         tc.tile_pool(name="inputs", bufs=UNITS) as inputs,
+        tc.tile_pool(name="regrouped", bufs=1) as regrouped,
         tc.tile_pool(name="quant", bufs=2) as quant,
         tc.tile_pool(name="moving", bufs=3) as moving,
-        tc.tile_pool(name="results", bufs=6) as results,
+        tc.tile_pool(name="results", bufs=10) as results,
         tc.psum_pool(name="psum_move", bufs=2) as psum_move,
-        tc.psum_pool(name="psum_mix", bufs=4) as psum_mix,
+        tc.psum_pool(name="psum_mix", bufs=2 * HALVES) as psum_mix,
+        tc.manual_schedule(),
     ):
         warm = consts.tile([P, 1], F32)
         nc.vector.memset(warm[:], 0.0)
@@ -52,120 +63,175 @@ def tile_spectralchannelmixing_t_e_kernel(tc, x, wc_words, wc_scales, out):
         nc.vector.memset(w_scales[:].bitcast(I32), 0)
         w_words = consts.tile([P, BLOCKS, 2 * CD], U8, align_bytes=64)
 
-        packed = []
-        resid = []
-        for u in range(UNITS):
-            b, i = divmod(u, BLOCKS)
-            unit_rows = x_rows[b, i * CD : (i + 1) * CD, :]
-            packed_u = inputs.tile([P, PACK, PIXELS], BF16, name="packed")
-            nc.sync.dma_start(out=packed_u[:], in_=unit_rows.rearrange("(p t) s -> p t s", t=PACK))
-            if u == 0:
-                nc.sync.dma_start(
-                    out=w_words[:].bitcast(I32),
-                    in_=wc_words.rearrange("g p n -> p g n").bitcast(I32),
-                )
-                for quad in range(4):
-                    nc.sync.dma_start(
-                        out=w_scales[32 * quad : 32 * quad + 4, :, :].bitcast(I32),
-                        in_=wc_scales[:, 4 * quad : 4 * quad + 4, :]
-                        .rearrange("g r n -> r g n")
-                        .bitcast(I32),
-                    )
-            resid_u = inputs.tile([P, M_TILES, PIXELS], BF16, name="resid")
+        def load_weights():
             nc.sync.dma_start(
-                out=resid_u[:, :LOADED_TILES, :],
-                in_=unit_rows[: LOADED_TILES * P, :].rearrange("(m q) s -> q m s", q=P),
+                out=w_words[:].bitcast(I32),
+                in_=wc_words.rearrange("g p n -> p g n").bitcast(I32),
             )
-            packed.append(packed_u)
-            resid.append(resid_u)
+            for quad in range(4):
+                nc.sync.dma_start(
+                    out=w_scales[32 * quad : 32 * quad + 4, :, :].bitcast(I32),
+                    in_=wc_scales[:, 4 * quad : 4 * quad + 4, :]
+                    .rearrange("g r n -> r g n")
+                    .bitcast(I32),
+                )
+
+        packed = {}
+        resid = {}
+        grouped = {}
+        x_codes = {}
+        x_scales = {}
+        by_pixel_ps = {}
+        by_pixel = {}
+        by_channel_ps = {}
+        acc = {}
+        result = {}
+
+        def load_packed(u):
+            b, i = divmod(u, BLOCKS)
+            packed[u] = inputs.tile([P, PACK, PIXELS], BF16, name="packed")
+            nc.sync.dma_start(
+                out=packed[u][:],
+                in_=x_rows[b, i * CD : (i + 1) * CD, :].rearrange("(p t) s -> p t s", t=PACK),
+            )
+
+        def load_residual(u):
+            b, i = divmod(u, BLOCKS)
+            resid[u] = inputs.tile([P, M_TILES, PIXELS], BF16, name="resid")
+            nc.sync.dma_start(
+                out=resid[u][:, :LOADED_TILES, :],
+                in_=x_rows[b, i * CD : i * CD + LOADED_TILES * P, :].rearrange(
+                    "(m q) s -> q m s", q=P
+                ),
+            )
 
         def regroup(u):
-            grouped = quant.tile([P, PIXELS, PACK], BF16, align_bytes=64, name="grouped")
+            grouped[u] = regrouped.tile([P, PIXELS, PACK], BF16, align_bytes=64, name="grouped")
             for half in range(HALVES):
                 s_cols = slice(half * N_TILE, (half + 1) * N_TILE)
-                nc.gpsimd.tensor_scalar(
-                    out=grouped[:, s_cols, :],
-                    in0=packed[u][:, :, s_cols].rearrange("p t s -> p s t"),
-                    scalar1=1.0,
-                    scalar2=0.0,
-                    op0=mybir.AluOpType.mult,
-                    op1=mybir.AluOpType.add,
-                )
-            return grouped
+                if u == 0:
+                    nc.vector.tensor_copy(
+                        out=grouped[u][:, s_cols, :].rearrange("p (c r) t -> p c t r", r=4),
+                        in_=packed[u][:, :, s_cols].rearrange("p t (c r) -> p c t r", r=4),
+                    )
+                else:
+                    nc.gpsimd.tensor_scalar(
+                        out=grouped[u][:, s_cols, :],
+                        in0=packed[u][:, :, s_cols].rearrange("p t s -> p s t"),
+                        scalar1=1.0,
+                        scalar2=0.0,
+                        op0=mybir.AluOpType.mult,
+                        op1=mybir.AluOpType.add,
+                    )
 
-        def move_residual(u):
-            packed_words = packed[u][:].bitcast(F32)
-            resid_words = resid[u][:].bitcast(F32)
-            for w0 in range(0, WORDS, P):
-                by_pixel_ps = psum_move.tile([P, PACK, P], F32, name="by_pixel_ps")
-                for t in range(PACK):
-                    nc.tensor.transpose(
-                        out=by_pixel_ps[:, t, :],
-                        in_=packed_words[:, t, w0 : w0 + P],
-                        identity=identity[:],
-                    )
-                by_pixel = moving.tile([P, MOVED_TILES * P], F32, name="by_pixel")
-                nc.scalar.copy(
-                    out=by_pixel[:].rearrange("v (p t) -> v p t", t=PACK),
-                    in_=by_pixel_ps[:, :, LOADED_TILES * P // PACK :].rearrange("v t p -> v p t"),
-                )
-                by_channel_ps = psum_move.tile([P, MOVED_TILES, P], F32, name="by_channel_ps")
-                for k in range(MOVED_TILES):
-                    nc.tensor.transpose(
-                        out=by_channel_ps[:, k, :],
-                        in_=by_pixel[:, k * P : (k + 1) * P],
-                        identity=identity[:],
-                    )
-                nc.vector.tensor_copy(
-                    out=resid_words[:, LOADED_TILES:, w0 : w0 + P], in_=by_channel_ps[:]
+        def quantise(u):
+            x_codes[u] = quant.tile([P, PIXELS], U32, align_bytes=64, name="x_codes")
+            x_scales[u] = quant.tile([P, PIXELS], U8, align_bytes=64, name="x_scales")
+            nc.vector.quantize_mx(
+                out=x_codes[u][:].bitcast(FP8X4),
+                scales=x_scales[u][:],
+                in_=grouped[u][:].rearrange("p s t -> p (s t)"),
+            )
+
+        def to_pixels(g):
+            u, k = divmod(g, GROUPS)
+            by_pixel_ps[g] = psum_move.tile([P, PACK, P], F32, name="by_pixel_ps")
+            for t in range(PACK):
+                nc.tensor.transpose(
+                    out=by_pixel_ps[g][:, t, :],
+                    in_=packed[u][:].bitcast(F32)[:, t, k * P : (k + 1) * P],
+                    identity=identity[:],
                 )
 
-        def mix(u, grouped):
-            b, i = divmod(u, BLOCKS)
-            x_codes = quant.tile([P, PIXELS], U32, align_bytes=64, name="x_codes")
-            x_scales = quant.tile([P, PIXELS], U8, align_bytes=64, name="x_scales")
+        def sort_channels(g):
+            by_pixel[g] = moving.tile([P, MOVED_TILES * P], F32, name="by_pixel")
+            nc.scalar.copy(
+                out=by_pixel[g][:].rearrange("v (p t) -> v p t", t=PACK),
+                in_=by_pixel_ps[g][:, :, LOADED_TILES * P // PACK :].rearrange("v t p -> v p t"),
+            )
+
+        def to_channels(g):
+            by_channel_ps[g] = psum_move.tile([P, MOVED_TILES, P], F32, name="by_channel_ps")
+            for j in range(MOVED_TILES):
+                nc.tensor.transpose(
+                    out=by_channel_ps[g][:, j, :],
+                    in_=by_pixel[g][:, j * P : (j + 1) * P],
+                    identity=identity[:],
+                )
+
+        def keep_residual(g):
+            u, k = divmod(g, GROUPS)
+            copy = nc.scalar.copy if g % 2 == 0 else nc.vector.tensor_copy
+            copy(
+                out=resid[u][:].bitcast(F32)[:, LOADED_TILES:, k * P : (k + 1) * P],
+                in_=by_channel_ps[g][:],
+            )
+
+        def multiply(n):
+            u, m = divmod(n, M_TILES)
+            i = u % BLOCKS
             for half in range(HALVES):
                 s_cols = slice(half * N_TILE, (half + 1) * N_TILE)
-                nc.vector.quantize_mx(
-                    out=x_codes[:, s_cols].bitcast(FP8X4),
-                    scales=x_scales[:, s_cols],
-                    in_=grouped[:, s_cols, :].rearrange("p s t -> p (s t)"),
+                acc[n, half] = psum_mix.tile([P, N_TILE], F32, name="acc")
+                nc.tensor.matmul_mx(
+                    out=acc[n, half][:],
+                    lhsT=w_words[:, i, 2 * P * m : 2 * P * (m + 1)].bitcast(FP4X4),
+                    lhsT_scale=w_scales[:, i, P * m : P * (m + 1)],
+                    rhs=x_codes[u][:, s_cols].bitcast(FP8X4),
+                    rhs_scale=x_scales[u][:, s_cols],
+                    start=True,
+                    stop=True,
                 )
-            unit_out = out_rows[b, i * CD : (i + 1) * CD, :].rearrange("(m q) s -> q m s", q=P)
-            for m0 in range(0, M_TILES, M_PAIR):
-                result = results.tile([P, M_PAIR, PIXELS], F32, name="result")
-                for k in range(M_PAIR):
-                    m = m0 + k
-                    for half in range(HALVES):
-                        s_cols = slice(half * N_TILE, (half + 1) * N_TILE)
-                        acc = psum_mix.tile([P, N_TILE], F32, name="acc")
-                        nc.tensor.matmul_mx(
-                            out=acc[:],
-                            lhsT=w_words[:, i, 2 * P * m : 2 * P * (m + 1)].bitcast(FP4X4),
-                            lhsT_scale=w_scales[:, i, P * m : P * (m + 1)],
-                            rhs=x_codes[:, s_cols].bitcast(FP8X4),
-                            rhs_scale=x_scales[:, s_cols],
-                            start=True,
-                            stop=True,
-                        )
-                        nc.vector.tensor_tensor(
-                            out=result[:, k, s_cols],
-                            in0=acc[:],
-                            in1=resid[u][:, m, s_cols],
-                            op=mybir.AluOpType.add,
-                        )
-                    nc.scalar.activation(
-                        out=result[:, k, :],
-                        in_=result[:, k, :],
-                        func=mybir.ActivationFunctionType.Gelu,
-                    )
-                nc.scalar.dma_start(out=unit_out[:, m0 : m0 + M_PAIR, :], in_=result[:])
 
-        grouped_next = regroup(0)
-        move_residual(0)
-        for u in range(UNITS):
-            grouped_now = grouped_next
-            if u + 1 < UNITS:
-                grouped_next = regroup(u + 1)
-                move_residual(u + 1)
-            mix(u, grouped_now)
+        def add_residual(n):
+            u, m = divmod(n, M_TILES)
+            result[n] = results.tile([P, PIXELS], F32, name="result")
+            for half in range(HALVES):
+                s_cols = slice(half * N_TILE, (half + 1) * N_TILE)
+                nc.vector.tensor_tensor(
+                    out=result[n][:, s_cols],
+                    in0=acc[n, half][:],
+                    in1=resid[u][:, m, s_cols],
+                    op=mybir.AluOpType.add,
+                )
+
+        def gelu_and_store(n):
+            b, c0 = divmod(n * P, BLOCKS * CD)
+            nc.scalar.activation(
+                out=result[n][:], in_=result[n][:], func=mybir.ActivationFunctionType.Gelu
+            )
+            nc.sync.dma_start(out=out_rows[b, c0 : c0 + P, :], in_=result[n][:])
+
+        def valid(index):
+            return 0 <= index < STEPS
+
+        load_packed(0)
+        load_weights()
+        load_residual(0)
+        for u in range(1, PREFETCH):
+            load_packed(u)
+            load_residual(u)
+        regroup(0)
+
+        for n in range(-TO_PIXELS_LEAD, STEPS + GELU_LAG):
+            if valid(n) and n % M_TILES == 0 and n // M_TILES + PREFETCH < UNITS:
+                load_packed(n // M_TILES + PREFETCH)
+                load_residual(n // M_TILES + PREFETCH)
+            if valid(n + TO_CHANNELS_LEAD):
+                to_channels(n + TO_CHANNELS_LEAD)
+            if valid(n + TO_PIXELS_LEAD):
+                to_pixels(n + TO_PIXELS_LEAD)
+            if valid(n):
+                multiply(n)
+            if valid(n - GELU_LAG):
+                gelu_and_store(n - GELU_LAG)
+            if valid(n - ADD_LAG):
+                add_residual(n - ADD_LAG)
+            if valid(n + KEEP_LEAD):
+                keep_residual(n + KEEP_LEAD)
+            if valid(n + SORT_LEAD):
+                sort_channels(n + SORT_LEAD)
+            if valid(n + 1) and (n + 1) % M_TILES == 0:
+                quantise((n + 1) // M_TILES)
+                if (n + 1) // M_TILES + 1 < UNITS:
+                    regroup((n + 1) // M_TILES + 1)

@@ -24,6 +24,7 @@ MOVED_TILES = M_TILES - LOADED_TILES
 WORDS = PIXELS // 2
 GROUPS = WORDS // P
 STEPS = UNITS * M_TILES
+SCALAR_PIXELS = 128
 PREFETCH = 3
 
 TO_PIXELS_LEAD = 4
@@ -107,22 +108,29 @@ def tile_spectralchannelmixing_t_e_kernel(tc, x, wc_words, wc_scales, out):
 
         def regroup(u):
             grouped[u] = regrouped.tile([P, PIXELS, PACK], BF16, align_bytes=64, name="grouped")
-            for half in range(HALVES):
-                s_cols = slice(half * N_TILE, (half + 1) * N_TILE)
+            piece = (PIXELS - SCALAR_PIXELS) // 2
+            for s0 in (0, piece):
                 if u == 0:
                     nc.vector.tensor_copy(
-                        out=grouped[u][:, s_cols, :].rearrange("p (c r) t -> p c t r", r=4),
-                        in_=packed[u][:, :, s_cols].rearrange("p t (c r) -> p c t r", r=4),
+                        out=grouped[u][:, s0 : s0 + piece, :].rearrange("p (c r) t -> p c t r", r=4),
+                        in_=packed[u][:, :, s0 : s0 + piece].rearrange("p t (c r) -> p c t r", r=4),
                     )
                 else:
                     nc.gpsimd.tensor_scalar(
-                        out=grouped[u][:, s_cols, :],
-                        in0=packed[u][:, :, s_cols].rearrange("p t s -> p s t"),
+                        out=grouped[u][:, s0 : s0 + piece, :],
+                        in0=packed[u][:, :, s0 : s0 + piece].rearrange("p t s -> p s t"),
                         scalar1=1.0,
                         scalar2=0.0,
                         op0=mybir.AluOpType.mult,
                         op1=mybir.AluOpType.add,
                     )
+
+        def regroup_rest(u):
+            s0 = PIXELS - SCALAR_PIXELS
+            nc.scalar.copy(
+                out=grouped[u][:, s0:, :].rearrange("p (c r) t -> p c t r", r=4),
+                in_=packed[u][:, :, s0:].rearrange("p t (c r) -> p c t r", r=4),
+            )
 
         def quantise(u):
             x_codes[u] = quant.tile([P, PIXELS], U32, align_bytes=64, name="x_codes")
@@ -212,6 +220,7 @@ def tile_spectralchannelmixing_t_e_kernel(tc, x, wc_words, wc_scales, out):
             load_packed(u)
             load_residual(u)
         regroup(0)
+        regroup_rest(0)
 
         for n in range(-TO_PIXELS_LEAD, STEPS + GELU_LAG):
             if valid(n) and n % M_TILES == 0 and n // M_TILES + PREFETCH < UNITS:
@@ -231,6 +240,8 @@ def tile_spectralchannelmixing_t_e_kernel(tc, x, wc_words, wc_scales, out):
                 keep_residual(n + KEEP_LEAD)
             if valid(n + SORT_LEAD):
                 sort_channels(n + SORT_LEAD)
+            if valid(n) and n % M_TILES == 0 and n // M_TILES + 1 < UNITS:
+                regroup_rest(n // M_TILES + 1)
             if valid(n + 1) and (n + 1) % M_TILES == 0:
                 quantise((n + 1) // M_TILES)
                 if (n + 1) // M_TILES + 1 < UNITS:

@@ -1,5 +1,4 @@
 import concourse.mybir as mybir
-from concourse.masks import make_identity
 
 BF16 = mybir.dt.bfloat16
 F32 = mybir.dt.float32
@@ -19,20 +18,11 @@ UNITS = BATCH * BLOCKS
 M_TILES = CD // P
 N_TILE = 512
 HALVES = PIXELS // N_TILE
-LOADED_TILES = 2
-MOVED_TILES = M_TILES - LOADED_TILES
-WORDS = PIXELS // 2
-GROUPS = WORDS // P
 STEPS = UNITS * M_TILES
-SCALAR_PIXELS = 128
-PREFETCH = 3
-
-TO_PIXELS_LEAD = 4
-SORT_LEAD = 3
-TO_CHANNELS_LEAD = 2
-KEEP_LEAD = 1
+SCALAR_PIXELS = 256
 ADD_LAG = 1
 GELU_LAG = 3
+RESULT_UNITS = 4
 
 FLOPS = 2 * BATCH * PIXELS * BLOCKS * CD * CD
 
@@ -47,44 +37,47 @@ def tile_spectralchannelmixing_t_e_kernel(tc, x, wc_words, wc_scales, out):
         tc.tile_pool(name="inputs", bufs=UNITS) as inputs,
         tc.tile_pool(name="regrouped", bufs=1) as regrouped,
         tc.tile_pool(name="quant", bufs=2) as quant,
-        tc.tile_pool(name="moving", bufs=3) as moving,
-        tc.tile_pool(name="results", bufs=10) as results,
-        tc.psum_pool(name="psum_move", bufs=2) as psum_move,
-        tc.psum_pool(name="psum_mix", bufs=2 * HALVES) as psum_mix,
+        tc.tile_pool(name="results", bufs=RESULT_UNITS) as results,
+        tc.psum_pool(name="psum_mix", bufs=4 * HALVES) as psum_mix,
         tc.manual_schedule(),
     ):
         warm = consts.tile([P, 1], F32)
         nc.vector.memset(warm[:], 0.0)
         nc.scalar.activation(out=warm[:], in_=warm[:], func=mybir.ActivationFunctionType.Gelu)
 
-        identity = consts.tile([P, P], F32)
-        make_identity(nc, identity[:])
-
-        w_scales = consts.tile([P, BLOCKS, CD], U8, align_bytes=64)
-        nc.vector.memset(w_scales[:].bitcast(I32), 0)
+        raw_words = consts.tile([P, BLOCKS, 2 * CD], U8)
+        raw_scales = consts.tile([P, BLOCKS, CD], U8)
+        nc.vector.memset(raw_scales[:].bitcast(I32), 0)
         w_words = consts.tile([P, BLOCKS, 2 * CD], U8, align_bytes=64)
+        w_scales = consts.tile([P, BLOCKS, CD], U8, align_bytes=64)
 
         def load_weights():
             nc.sync.dma_start(
-                out=w_words[:].bitcast(I32),
+                out=raw_words[:].bitcast(I32),
                 in_=wc_words.rearrange("g p n -> p g n").bitcast(I32),
             )
             for quad in range(4):
                 nc.sync.dma_start(
-                    out=w_scales[32 * quad : 32 * quad + 4, :, :].bitcast(I32),
+                    out=raw_scales[32 * quad : 32 * quad + 4, :, :].bitcast(I32),
                     in_=wc_scales[:, 4 * quad : 4 * quad + 4, :]
                     .rearrange("g r n -> r g n")
                     .bitcast(I32),
                 )
 
+        def sort_columns(i):
+            nc.vector.tensor_copy(
+                out=w_words[:, i, :].rearrange("p (t q b) -> p t q b", t=M_TILES, b=2),
+                in_=raw_words[:, i, :].rearrange("p (q t b) -> p t q b", t=M_TILES, b=2),
+            )
+            nc.vector.tensor_copy(
+                out=w_scales[:, i, :].rearrange("p (t q) -> p t q", t=M_TILES),
+                in_=raw_scales[:, i, :].rearrange("p (q t) -> p t q", t=M_TILES),
+            )
+
         packed = {}
-        resid = {}
         grouped = {}
         x_codes = {}
         x_scales = {}
-        by_pixel_ps = {}
-        by_pixel = {}
-        by_channel_ps = {}
         acc = {}
         result = {}
 
@@ -94,16 +87,6 @@ def tile_spectralchannelmixing_t_e_kernel(tc, x, wc_words, wc_scales, out):
             nc.sync.dma_start(
                 out=packed[u][:],
                 in_=x_rows[b, i * CD : (i + 1) * CD, :].rearrange("(p t) s -> p t s", t=PACK),
-            )
-
-        def load_residual(u):
-            b, i = divmod(u, BLOCKS)
-            resid[u] = inputs.tile([P, M_TILES, PIXELS], BF16, name="resid")
-            nc.sync.dma_start(
-                out=resid[u][:, :LOADED_TILES, :],
-                in_=x_rows[b, i * CD : i * CD + LOADED_TILES * P, :].rearrange(
-                    "(m q) s -> q m s", q=P
-                ),
             )
 
         def regroup(u):
@@ -141,50 +124,16 @@ def tile_spectralchannelmixing_t_e_kernel(tc, x, wc_words, wc_scales, out):
                 in_=grouped[u][:].rearrange("p s t -> p (s t)"),
             )
 
-        def to_pixels(g):
-            u, k = divmod(g, GROUPS)
-            by_pixel_ps[g] = psum_move.tile([P, PACK, P], F32, name="by_pixel_ps")
-            for t in range(PACK):
-                nc.tensor.transpose(
-                    out=by_pixel_ps[g][:, t, :],
-                    in_=packed[u][:].bitcast(F32)[:, t, k * P : (k + 1) * P],
-                    identity=identity[:],
-                )
-
-        def sort_channels(g):
-            by_pixel[g] = moving.tile([P, MOVED_TILES * P], F32, name="by_pixel")
-            nc.scalar.copy(
-                out=by_pixel[g][:].rearrange("v (p t) -> v p t", t=PACK),
-                in_=by_pixel_ps[g][:, :, LOADED_TILES * P // PACK :].rearrange("v t p -> v p t"),
-            )
-
-        def to_channels(g):
-            by_channel_ps[g] = psum_move.tile([P, MOVED_TILES, P], F32, name="by_channel_ps")
-            for j in range(MOVED_TILES):
-                nc.tensor.transpose(
-                    out=by_channel_ps[g][:, j, :],
-                    in_=by_pixel[g][:, j * P : (j + 1) * P],
-                    identity=identity[:],
-                )
-
-        def keep_residual(g):
-            u, k = divmod(g, GROUPS)
-            copy = nc.scalar.copy if g % 2 == 0 else nc.vector.tensor_copy
-            copy(
-                out=resid[u][:].bitcast(F32)[:, LOADED_TILES:, k * P : (k + 1) * P],
-                in_=by_channel_ps[g][:],
-            )
-
         def multiply(n):
-            u, m = divmod(n, M_TILES)
+            u, t = divmod(n, M_TILES)
             i = u % BLOCKS
             for half in range(HALVES):
                 s_cols = slice(half * N_TILE, (half + 1) * N_TILE)
                 acc[n, half] = psum_mix.tile([P, N_TILE], F32, name="acc")
                 nc.tensor.matmul_mx(
                     out=acc[n, half][:],
-                    lhsT=w_words[:, i, 2 * P * m : 2 * P * (m + 1)].bitcast(FP4X4),
-                    lhsT_scale=w_scales[:, i, P * m : P * (m + 1)],
+                    lhsT=w_words[:, i, 2 * P * t : 2 * P * (t + 1)].bitcast(FP4X4),
+                    lhsT_scale=w_scales[:, i, P * t : P * (t + 1)],
                     rhs=x_codes[u][:, s_cols].bitcast(FP8X4),
                     rhs_scale=x_scales[u][:, s_cols],
                     start=True,
@@ -192,54 +141,51 @@ def tile_spectralchannelmixing_t_e_kernel(tc, x, wc_words, wc_scales, out):
                 )
 
         def add_residual(n):
-            u, m = divmod(n, M_TILES)
-            result[n] = results.tile([P, PIXELS], F32, name="result")
+            u, t = divmod(n, M_TILES)
+            if t == 0:
+                result[u] = results.tile([P, M_TILES, PIXELS], F32, name="result")
             for half in range(HALVES):
                 s_cols = slice(half * N_TILE, (half + 1) * N_TILE)
                 nc.vector.tensor_tensor(
-                    out=result[n][:, s_cols],
+                    out=result[u][:, t, s_cols],
                     in0=acc[n, half][:],
-                    in1=resid[u][:, m, s_cols],
+                    in1=packed[u][:, t, s_cols],
                     op=mybir.AluOpType.add,
                 )
 
         def gelu_and_store(n):
-            b, c0 = divmod(n * P, BLOCKS * CD)
+            u, t = divmod(n, M_TILES)
+            b, i = divmod(u, BLOCKS)
             nc.scalar.activation(
-                out=result[n][:], in_=result[n][:], func=mybir.ActivationFunctionType.Gelu
+                out=result[u][:, t, :],
+                in_=result[u][:, t, :],
+                func=mybir.ActivationFunctionType.Gelu,
             )
-            nc.sync.dma_start(out=out_rows[b, c0 : c0 + P, :], in_=result[n][:])
+            nc.sync.dma_start(
+                out=out_rows[b, i * CD : (i + 1) * CD, :].rearrange("(q t) s -> q t s", t=M_TILES)[
+                    :, t, :
+                ],
+                in_=result[u][:, t, :],
+            )
 
         def valid(index):
             return 0 <= index < STEPS
 
-        load_packed(0)
         load_weights()
-        load_residual(0)
-        for u in range(1, PREFETCH):
+        for u in range(UNITS):
             load_packed(u)
-            load_residual(u)
+        for i in range(BLOCKS):
+            sort_columns(i)
         regroup(0)
         regroup_rest(0)
 
-        for n in range(-TO_PIXELS_LEAD, STEPS + GELU_LAG):
-            if valid(n) and n % M_TILES == 0 and n // M_TILES + PREFETCH < UNITS:
-                load_packed(n // M_TILES + PREFETCH)
-                load_residual(n // M_TILES + PREFETCH)
-            if valid(n + TO_CHANNELS_LEAD):
-                to_channels(n + TO_CHANNELS_LEAD)
-            if valid(n + TO_PIXELS_LEAD):
-                to_pixels(n + TO_PIXELS_LEAD)
+        for n in range(-1, STEPS + GELU_LAG):
             if valid(n):
                 multiply(n)
             if valid(n - GELU_LAG):
                 gelu_and_store(n - GELU_LAG)
             if valid(n - ADD_LAG):
                 add_residual(n - ADD_LAG)
-            if valid(n + KEEP_LEAD):
-                keep_residual(n + KEEP_LEAD)
-            if valid(n + SORT_LEAD):
-                sort_channels(n + SORT_LEAD)
             if valid(n) and n % M_TILES == 0 and n // M_TILES + 1 < UNITS:
                 regroup_rest(n // M_TILES + 1)
             if valid(n + 1) and (n + 1) % M_TILES == 0:

@@ -18,11 +18,18 @@ UNITS = BATCH * BLOCKS
 M_TILES = CD // P
 N_TILE = 512
 HALVES = PIXELS // N_TILE
-STEPS = UNITS * M_TILES
-SCALAR_PIXELS = 256
+PIECE = 384
+SCALAR_SHARE = 4
 ADD_LAG = 1
 GELU_LAG = 3
 RESULT_UNITS = 4
+
+CHUNKS = [(0, half * N_TILE, N_TILE) for half in range(HALVES)] + [
+    (u, 0, PIXELS) for u in range(1, UNITS)
+]
+STEPS = [(c, t) for c in range(len(CHUNKS)) for t in range(M_TILES)]
+QUANT_LEAD = [3 if pixels < PIXELS else 1 for (u, s0, pixels) in CHUNKS]
+SORT_ROUND = 2
 
 FLOPS = 2 * BATCH * PIXELS * BLOCKS * CD * CD
 
@@ -34,7 +41,8 @@ def tile_spectralchannelmixing_t_e_kernel(tc, x, wc_words, wc_scales, out):
 
     with (
         tc.tile_pool(name="consts", bufs=1) as consts,
-        tc.tile_pool(name="inputs", bufs=UNITS) as inputs,
+        tc.tile_pool(name="inputs", bufs=UNITS - 1) as inputs,
+        tc.tile_pool(name="first_inputs", bufs=HALVES) as first_inputs,
         tc.tile_pool(name="regrouped", bufs=1) as regrouped,
         tc.tile_pool(name="quant", bufs=2) as quant,
         tc.tile_pool(name="results", bufs=RESULT_UNITS) as results,
@@ -64,11 +72,13 @@ def tile_spectralchannelmixing_t_e_kernel(tc, x, wc_words, wc_scales, out):
                     .bitcast(I32),
                 )
 
-        def sort_columns(i):
+        def sort_words(i):
             nc.vector.tensor_copy(
                 out=w_words[:, i, :].rearrange("p (t q b) -> p t q b", t=M_TILES, b=2),
                 in_=raw_words[:, i, :].rearrange("p (q t b) -> p t q b", t=M_TILES, b=2),
             )
+
+        def sort_scales(i):
             nc.vector.tensor_copy(
                 out=w_scales[:, i, :].rearrange("p (t q) -> p t q", t=M_TILES),
                 in_=raw_scales[:, i, :].rearrange("p (q t) -> p t q", t=M_TILES),
@@ -81,114 +91,139 @@ def tile_spectralchannelmixing_t_e_kernel(tc, x, wc_words, wc_scales, out):
         acc = {}
         result = {}
 
-        def load_packed(u):
+        def load_packed(c):
+            u, s0, pixels = CHUNKS[c]
             b, i = divmod(u, BLOCKS)
-            packed[u] = inputs.tile([P, PACK, PIXELS], BF16, name="packed")
+            pool = inputs if pixels == PIXELS else first_inputs
+            packed[c] = pool.tile([P, PACK, pixels], BF16, name="packed")
             nc.sync.dma_start(
-                out=packed[u][:],
-                in_=x_rows[b, i * CD : (i + 1) * CD, :].rearrange("(p t) s -> p t s", t=PACK),
+                out=packed[c][:],
+                in_=x_rows[b, i * CD : (i + 1) * CD, s0 : s0 + pixels].rearrange(
+                    "(p t) s -> p t s", t=PACK
+                ),
             )
 
-        def regroup(u):
-            grouped[u] = regrouped.tile([P, PIXELS, PACK], BF16, align_bytes=64, name="grouped")
-            piece = (PIXELS - SCALAR_PIXELS) // 2
-            for s0 in (0, piece):
+        def regroup(c):
+            u, s0, pixels = CHUNKS[c]
+            if s0 == 0:
+                grouped[u] = regrouped.tile([P, PIXELS, PACK], BF16, align_bytes=64, name="grouped")
+            for p0 in range(s0, s0 + pixels - pixels // SCALAR_SHARE, PIECE):
                 if u == 0:
                     nc.vector.tensor_copy(
-                        out=grouped[u][:, s0 : s0 + piece, :].rearrange("p (c r) t -> p c t r", r=4),
-                        in_=packed[u][:, :, s0 : s0 + piece].rearrange("p t (c r) -> p c t r", r=4),
+                        out=grouped[u][:, p0 : p0 + PIECE, :].rearrange("p (c r) t -> p c t r", r=4),
+                        in_=packed[c][:, :, p0 - s0 : p0 - s0 + PIECE].rearrange(
+                            "p t (c r) -> p c t r", r=4
+                        ),
                     )
                 else:
                     nc.gpsimd.tensor_scalar(
-                        out=grouped[u][:, s0 : s0 + piece, :],
-                        in0=packed[u][:, :, s0 : s0 + piece].rearrange("p t s -> p s t"),
+                        out=grouped[u][:, p0 : p0 + PIECE, :],
+                        in0=packed[c][:, :, p0 - s0 : p0 - s0 + PIECE].rearrange("p t s -> p s t"),
                         scalar1=1.0,
                         scalar2=0.0,
                         op0=mybir.AluOpType.mult,
                         op1=mybir.AluOpType.add,
                     )
 
-        def regroup_rest(u):
-            s0 = PIXELS - SCALAR_PIXELS
+        def regroup_rest(c):
+            u, s0, pixels = CHUNKS[c]
+            r0 = pixels - pixels // SCALAR_SHARE
             nc.scalar.copy(
-                out=grouped[u][:, s0:, :].rearrange("p (c r) t -> p c t r", r=4),
-                in_=packed[u][:, :, s0:].rearrange("p t (c r) -> p c t r", r=4),
+                out=grouped[u][:, s0 + r0 : s0 + pixels, :].rearrange("p (c r) t -> p c t r", r=4),
+                in_=packed[c][:, :, r0:].rearrange("p t (c r) -> p c t r", r=4),
             )
 
-        def quantise(u):
-            x_codes[u] = quant.tile([P, PIXELS], U32, align_bytes=64, name="x_codes")
-            x_scales[u] = quant.tile([P, PIXELS], U8, align_bytes=64, name="x_scales")
+        def quantise(c):
+            u, s0, pixels = CHUNKS[c]
+            if s0 == 0:
+                x_codes[u] = quant.tile([P, PIXELS], U32, align_bytes=64, name="x_codes")
+                x_scales[u] = quant.tile([P, PIXELS], U8, align_bytes=64, name="x_scales")
             nc.vector.quantize_mx(
-                out=x_codes[u][:].bitcast(FP8X4),
-                scales=x_scales[u][:],
-                in_=grouped[u][:].rearrange("p s t -> p (s t)"),
+                out=x_codes[u][:, s0 : s0 + pixels].bitcast(FP8X4),
+                scales=x_scales[u][:, s0 : s0 + pixels],
+                in_=grouped[u][:, s0 : s0 + pixels, :].rearrange("p s t -> p (s t)"),
             )
 
-        def multiply(n):
-            u, t = divmod(n, M_TILES)
+        def multiply(k):
+            c, t = STEPS[k]
+            u, s0, pixels = CHUNKS[c]
             i = u % BLOCKS
-            for half in range(HALVES):
-                s_cols = slice(half * N_TILE, (half + 1) * N_TILE)
-                acc[n, half] = psum_mix.tile([P, N_TILE], F32, name="acc")
+            for h0 in range(s0, s0 + pixels, N_TILE):
+                acc[k, h0] = psum_mix.tile([P, N_TILE], F32, name="acc")
                 nc.tensor.matmul_mx(
-                    out=acc[n, half][:],
+                    out=acc[k, h0][:],
                     lhsT=w_words[:, i, 2 * P * t : 2 * P * (t + 1)].bitcast(FP4X4),
                     lhsT_scale=w_scales[:, i, P * t : P * (t + 1)],
-                    rhs=x_codes[u][:, s_cols].bitcast(FP8X4),
-                    rhs_scale=x_scales[u][:, s_cols],
+                    rhs=x_codes[u][:, h0 : h0 + N_TILE].bitcast(FP8X4),
+                    rhs_scale=x_scales[u][:, h0 : h0 + N_TILE],
                     start=True,
                     stop=True,
                 )
 
-        def add_residual(n):
-            u, t = divmod(n, M_TILES)
-            if t == 0:
+        def add_residual(k):
+            c, t = STEPS[k]
+            u, s0, pixels = CHUNKS[c]
+            if t == 0 and s0 == 0:
                 result[u] = results.tile([P, M_TILES, PIXELS], F32, name="result")
-            for half in range(HALVES):
-                s_cols = slice(half * N_TILE, (half + 1) * N_TILE)
+            for h0 in range(s0, s0 + pixels, N_TILE):
                 nc.vector.tensor_tensor(
-                    out=result[u][:, t, s_cols],
-                    in0=acc[n, half][:],
-                    in1=packed[u][:, t, s_cols],
+                    out=result[u][:, t, h0 : h0 + N_TILE],
+                    in0=acc[k, h0][:],
+                    in1=packed[c][:, t, h0 - s0 : h0 - s0 + N_TILE],
                     op=mybir.AluOpType.add,
                 )
 
-        def gelu_and_store(n):
-            u, t = divmod(n, M_TILES)
+        def store(u, t, s0, pixels):
             b, i = divmod(u, BLOCKS)
-            nc.scalar.activation(
-                out=result[u][:, t, :],
-                in_=result[u][:, t, :],
-                func=mybir.ActivationFunctionType.Gelu,
-            )
             nc.sync.dma_start(
-                out=out_rows[b, i * CD : (i + 1) * CD, :].rearrange("(q t) s -> q t s", t=M_TILES)[
-                    :, t, :
-                ],
-                in_=result[u][:, t, :],
+                out=out_rows[b, i * CD : (i + 1) * CD, s0 : s0 + pixels].rearrange(
+                    "(q t) s -> q t s", t=M_TILES
+                )[:, t, :],
+                in_=result[u][:, t, s0 : s0 + pixels],
             )
 
-        def valid(index):
-            return 0 <= index < STEPS
+        def gelu_and_store(k):
+            c, t = STEPS[k]
+            u, s0, pixels = CHUNKS[c]
+            last = k == len(STEPS) - 1
+            width = N_TILE if last else pixels
+            for g0 in range(s0, s0 + pixels, width):
+                nc.scalar.activation(
+                    out=result[u][:, t, g0 : g0 + width],
+                    in_=result[u][:, t, g0 : g0 + width],
+                    func=mybir.ActivationFunctionType.Gelu,
+                )
+                if last:
+                    store(u, t, g0, width)
+            if not last and s0 + pixels == PIXELS:
+                store(u, t, 0, PIXELS)
+
+        def valid(k):
+            return 0 <= k < len(STEPS)
 
         load_weights()
-        for u in range(UNITS):
-            load_packed(u)
-        for i in range(BLOCKS):
-            sort_columns(i)
+        for c in range(len(CHUNKS)):
+            load_packed(c)
+        sort_words(0)
+        sort_scales(0)
         regroup(0)
         regroup_rest(0)
+        sort_scales(1)
 
-        for n in range(-1, STEPS + GELU_LAG):
-            if valid(n):
-                multiply(n)
-            if valid(n - GELU_LAG):
-                gelu_and_store(n - GELU_LAG)
-            if valid(n - ADD_LAG):
-                add_residual(n - ADD_LAG)
-            if valid(n) and n % M_TILES == 0 and n // M_TILES + 1 < UNITS:
-                regroup_rest(n // M_TILES + 1)
-            if valid(n + 1) and (n + 1) % M_TILES == 0:
-                quantise((n + 1) // M_TILES)
-                if (n + 1) // M_TILES + 1 < UNITS:
-                    regroup((n + 1) // M_TILES + 1)
+        quant_round = {c * M_TILES - QUANT_LEAD[c]: c for c in range(len(CHUNKS))}
+
+        for k in range(-QUANT_LEAD[0], len(STEPS) + GELU_LAG):
+            if valid(k):
+                multiply(k)
+            if valid(k - GELU_LAG):
+                gelu_and_store(k - GELU_LAG)
+            if valid(k - ADD_LAG):
+                add_residual(k - ADD_LAG)
+            if k == SORT_ROUND:
+                sort_words(1)
+            if k - 1 in quant_round and quant_round[k - 1] + 1 < len(CHUNKS):
+                regroup_rest(quant_round[k - 1] + 1)
+            if k in quant_round:
+                quantise(quant_round[k])
+                if quant_round[k] + 1 < len(CHUNKS):
+                    regroup(quant_round[k] + 1)

@@ -1,4 +1,5 @@
 import concourse.mybir as mybir
+from concourse.masks import make_identity
 
 BF16 = mybir.dt.bfloat16
 F32 = mybir.dt.float32
@@ -18,8 +19,10 @@ UNITS = BATCH * BLOCKS
 M_TILES = CD // P
 N_TILE = 512
 HALVES = PIXELS // N_TILE
-PIECE = 384
-SCALAR_SHARE = 4
+FIRST_SCALAR_PIXELS = 128
+TENSOR_PIXELS = 384
+TURN_PIXELS = P
+BANK_PIXELS = 256
 ADD_LAG = 1
 GELU_LAG = 3
 RESULT_UNITS = 4
@@ -46,12 +49,16 @@ def tile_spectralchannelmixing_t_e_kernel(tc, x, wc_words, wc_scales, out):
         tc.tile_pool(name="regrouped", bufs=1) as regrouped,
         tc.tile_pool(name="quant", bufs=2) as quant,
         tc.tile_pool(name="results", bufs=RESULT_UNITS) as results,
-        tc.psum_pool(name="psum_mix", bufs=4 * HALVES) as psum_mix,
+        tc.psum_pool(name="psum_mix", bufs=3 * HALVES) as psum_mix,
+        tc.psum_pool(name="psum_turn", bufs=2) as psum_turn,
         tc.manual_schedule(),
     ):
         warm = consts.tile([P, 1], F32)
         nc.vector.memset(warm[:], 0.0)
         nc.scalar.activation(out=warm[:], in_=warm[:], func=mybir.ActivationFunctionType.Gelu)
+
+        identity = consts.tile([P, P], BF16)
+        make_identity(nc, identity[:])
 
         raw_words = consts.tile([P, BLOCKS, 2 * CD], U8)
         raw_scales = consts.tile([P, BLOCKS, CD], U8)
@@ -86,6 +93,7 @@ def tile_spectralchannelmixing_t_e_kernel(tc, x, wc_words, wc_scales, out):
 
         packed = {}
         grouped = {}
+        turned = {}
         x_codes = {}
         x_scales = {}
         acc = {}
@@ -107,31 +115,56 @@ def tile_spectralchannelmixing_t_e_kernel(tc, x, wc_words, wc_scales, out):
             u, s0, pixels = CHUNKS[c]
             if s0 == 0:
                 grouped[u] = regrouped.tile([P, PIXELS, PACK], BF16, align_bytes=64, name="grouped")
-            for p0 in range(s0, s0 + pixels - pixels // SCALAR_SHARE, PIECE):
-                if u == 0:
-                    nc.vector.tensor_copy(
-                        out=grouped[u][:, p0 : p0 + PIECE, :].rearrange("p (c r) t -> p c t r", r=4),
-                        in_=packed[c][:, :, p0 - s0 : p0 - s0 + PIECE].rearrange(
-                            "p t (c r) -> p c t r", r=4
-                        ),
-                    )
-                else:
+            if u == 0:
+                share = pixels - FIRST_SCALAR_PIXELS
+                nc.vector.tensor_copy(
+                    out=grouped[u][:, s0 : s0 + share, :].rearrange("p (c r) t -> p c t r", r=4),
+                    in_=packed[c][:, :, :share].rearrange("p t (c r) -> p c t r", r=4),
+                )
+            else:
+                piece = (pixels - TENSOR_PIXELS) // 2
+                for p0 in (0, piece):
                     nc.gpsimd.tensor_scalar(
-                        out=grouped[u][:, p0 : p0 + PIECE, :],
-                        in0=packed[c][:, :, p0 - s0 : p0 - s0 + PIECE].rearrange("p t s -> p s t"),
+                        out=grouped[u][:, p0 : p0 + piece, :],
+                        in0=packed[c][:, :, p0 : p0 + piece].rearrange("p t s -> p s t"),
                         scalar1=1.0,
                         scalar2=0.0,
                         op0=mybir.AluOpType.mult,
                         op1=mybir.AluOpType.add,
                     )
 
+        def turn(c):
+            u, s0, pixels = CHUNKS[c]
+            for p0 in range(pixels - TENSOR_PIXELS, pixels, TURN_PIXELS):
+                bank, place = divmod(p0 - (pixels - TENSOR_PIXELS), BANK_PIXELS)
+                if place == 0:
+                    turned[c, bank] = psum_turn.tile([P, BANK_PIXELS * PACK], BF16, name="turned")
+                nc.tensor.matmul(
+                    out=turned[c, bank][:, place * PACK : (place + TURN_PIXELS) * PACK],
+                    lhsT=identity[:],
+                    rhs=packed[c][:, :, p0 : p0 + TURN_PIXELS].rearrange("p t s -> p s t"),
+                    start=True,
+                    stop=True,
+                )
+
         def regroup_rest(c):
             u, s0, pixels = CHUNKS[c]
-            r0 = pixels - pixels // SCALAR_SHARE
-            nc.scalar.copy(
-                out=grouped[u][:, s0 + r0 : s0 + pixels, :].rearrange("p (c r) t -> p c t r", r=4),
-                in_=packed[c][:, :, r0:].rearrange("p t (c r) -> p c t r", r=4),
-            )
+            if u == 0:
+                r0 = pixels - FIRST_SCALAR_PIXELS
+                nc.scalar.copy(
+                    out=grouped[u][:, s0 + r0 : s0 + pixels, :].rearrange(
+                        "p (c r) t -> p c t r", r=4
+                    ),
+                    in_=packed[c][:, :, r0:].rearrange("p t (c r) -> p c t r", r=4),
+                )
+            else:
+                for p0 in range(pixels - TENSOR_PIXELS, pixels, BANK_PIXELS):
+                    width = min(BANK_PIXELS, pixels - p0)
+                    bank = (p0 - (pixels - TENSOR_PIXELS)) // BANK_PIXELS
+                    nc.scalar.copy(
+                        out=grouped[u][:, p0 : p0 + width, :].rearrange("p s t -> p (s t)"),
+                        in_=turned[c, bank][:, : width * PACK],
+                    )
 
         def quantise(c):
             u, s0, pixels = CHUNKS[c]
@@ -215,14 +248,17 @@ def tile_spectralchannelmixing_t_e_kernel(tc, x, wc_words, wc_scales, out):
         for k in range(-QUANT_LEAD[0], len(STEPS) + GELU_LAG):
             if valid(k):
                 multiply(k)
+            if valid(k + 1) and STEPS[k + 1][1] == 0 and STEPS[k + 1][0] + 1 < len(CHUNKS):
+                if CHUNKS[STEPS[k + 1][0] + 1][0] > 0:
+                    turn(STEPS[k + 1][0] + 1)
             if valid(k - GELU_LAG):
                 gelu_and_store(k - GELU_LAG)
             if valid(k - ADD_LAG):
                 add_residual(k - ADD_LAG)
             if k == SORT_ROUND:
                 sort_words(1)
-            if k - 1 in quant_round and quant_round[k - 1] + 1 < len(CHUNKS):
-                regroup_rest(quant_round[k - 1] + 1)
+            if valid(k) and STEPS[k][1] == 0 and STEPS[k][0] + 1 < len(CHUNKS):
+                regroup_rest(STEPS[k][0] + 1)
             if k in quant_round:
                 quantise(quant_round[k])
                 if quant_round[k] + 1 < len(CHUNKS):

@@ -26,6 +26,7 @@ BANK_PIXELS = 256
 ADD_LAG = 1
 GELU_LAG = 3
 RESULT_UNITS = 4
+STORE_ROWS = 2
 
 CHUNKS = [(0, half * N_TILE, N_TILE) for half in range(HALVES)] + [
     (u, 0, PIXELS) for u in range(1, UNITS)
@@ -206,13 +207,13 @@ def tile_spectralchannelmixing_t_e_kernel(tc, x, wc_words, wc_scales, out):
                     op=mybir.AluOpType.add,
                 )
 
-        def store(u, t, s0, pixels):
+        def store(u, t, rows, s0, pixels):
             b, i = divmod(u, BLOCKS)
             nc.sync.dma_start(
                 out=out_rows[b, i * CD : (i + 1) * CD, s0 : s0 + pixels].rearrange(
                     "(q t) s -> q t s", t=M_TILES
-                )[:, t, :],
-                in_=result[u][:, t, s0 : s0 + pixels],
+                )[:, t : t + rows, :],
+                in_=result[u][:, t : t + rows, s0 : s0 + pixels],
             )
 
         def gelu_and_store(k):
@@ -227,9 +228,10 @@ def tile_spectralchannelmixing_t_e_kernel(tc, x, wc_words, wc_scales, out):
                     func=mybir.ActivationFunctionType.Gelu,
                 )
                 if last:
-                    store(u, t, g0, width)
-            if not last and s0 + pixels == PIXELS:
-                store(u, t, 0, PIXELS)
+                    store(u, t, 1, g0, width)
+            rows = 1 if u == UNITS - 1 else STORE_ROWS
+            if not last and s0 + pixels == PIXELS and (t + 1) % rows == 0:
+                store(u, t + 1 - rows, rows, 0, PIXELS)
 
         def valid(k):
             return 0 <= k < len(STEPS)

@@ -32,8 +32,8 @@ CHUNKS = [(0, half * N_TILE, N_TILE) for half in range(HALVES)] + [
     (u, 0, PIXELS) for u in range(1, UNITS)
 ]
 STEPS = [(c, t) for c in range(len(CHUNKS)) for t in range(M_TILES)]
-QUANT_LEAD = [3 if pixels < PIXELS else 1 for (u, s0, pixels) in CHUNKS]
-SORT_ROUND = 2
+QUANT_LEAD = [3, 3, 1] + [2] * (UNITS - 2)
+SORT_ROUND = -2
 
 FLOPS = 2 * BATCH * PIXELS * BLOCKS * CD * CD
 

@@ -19,7 +19,7 @@ UNITS = BATCH * BLOCKS
 M_TILES = CD // P
 N_TILE = 512
 HALVES = PIXELS // N_TILE
-FIRST_SCALAR_PIXELS = 128
+FIRST_SCALAR_PIXELS = (128, 512)
 TENSOR_PIXELS = 384
 TURN_PIXELS = P
 BANK_PIXELS = 256
@@ -117,11 +117,14 @@ def tile_spectralchannelmixing_t_e_kernel(tc, x, wc_words, wc_scales, out):
             if s0 == 0:
                 grouped[u] = regrouped.tile([P, PIXELS, PACK], BF16, align_bytes=64, name="grouped")
             if u == 0:
-                share = pixels - FIRST_SCALAR_PIXELS
-                nc.vector.tensor_copy(
-                    out=grouped[u][:, s0 : s0 + share, :].rearrange("p (c r) t -> p c t r", r=4),
-                    in_=packed[c][:, :, :share].rearrange("p t (c r) -> p c t r", r=4),
-                )
+                share = pixels - FIRST_SCALAR_PIXELS[c]
+                if share > 0:
+                    nc.vector.tensor_copy(
+                        out=grouped[u][:, s0 : s0 + share, :].rearrange(
+                            "p (c r) t -> p c t r", r=4
+                        ),
+                        in_=packed[c][:, :, :share].rearrange("p t (c r) -> p c t r", r=4),
+                    )
             else:
                 piece = (pixels - TENSOR_PIXELS) // 2
                 for p0 in (0, piece):
@@ -151,7 +154,7 @@ def tile_spectralchannelmixing_t_e_kernel(tc, x, wc_words, wc_scales, out):
         def regroup_rest(c):
             u, s0, pixels = CHUNKS[c]
             if u == 0:
-                r0 = pixels - FIRST_SCALAR_PIXELS
+                r0 = pixels - FIRST_SCALAR_PIXELS[c]
                 nc.scalar.copy(
                     out=grouped[u][:, s0 + r0 : s0 + pixels, :].rearrange(
                         "p (c r) t -> p c t r", r=4

@@ -19,13 +19,13 @@ UNITS = BATCH * BLOCKS
 M_TILES = CD // P
 N_TILE = 512
 HALVES = PIXELS // N_TILE
-FIRST_SCALAR_PIXELS = (128, 512)
+FIRST_SCALAR_PIXELS = (128, 128)
 TENSOR_PIXELS = 384
 TURN_PIXELS = P
 BANK_PIXELS = 256
 ADD_LAG = 1
 GELU_LAG = 3
-RESULT_UNITS = 4
+RESULT_UNITS = 6
 STORE_ROWS = 2
 
 CHUNKS = [(0, half * N_TILE, N_TILE) for half in range(HALVES)] + [
@@ -33,7 +33,6 @@ CHUNKS = [(0, half * N_TILE, N_TILE) for half in range(HALVES)] + [
 ]
 STEPS = [(c, t) for c in range(len(CHUNKS)) for t in range(M_TILES)]
 QUANT_LEAD = [3, 3, 1] + [2] * (UNITS - 2)
-SORT_ROUND = -2
 
 FLOPS = 2 * BATCH * PIXELS * BLOCKS * CD * CD
 
@@ -48,7 +47,7 @@ def tile_spectralchannelmixing_t_e_kernel(tc, x, wc_words, wc_scales, out):
         tc.tile_pool(name="inputs", bufs=UNITS - 1) as inputs,
         tc.tile_pool(name="first_inputs", bufs=HALVES) as first_inputs,
         tc.tile_pool(name="regrouped", bufs=1) as regrouped,
-        tc.tile_pool(name="quant", bufs=2) as quant,
+        tc.tile_pool(name="quant", bufs=UNITS) as quant,
         tc.tile_pool(name="results", bufs=RESULT_UNITS) as results,
         tc.psum_pool(name="psum_mix", bufs=3 * HALVES) as psum_mix,
         tc.psum_pool(name="psum_turn", bufs=2) as psum_turn,
@@ -126,16 +125,15 @@ def tile_spectralchannelmixing_t_e_kernel(tc, x, wc_words, wc_scales, out):
                         in_=packed[c][:, :, :share].rearrange("p t (c r) -> p c t r", r=4),
                     )
             else:
-                piece = (pixels - TENSOR_PIXELS) // 2
-                for p0 in (0, piece):
-                    nc.gpsimd.tensor_scalar(
-                        out=grouped[u][:, p0 : p0 + piece, :],
-                        in0=packed[c][:, :, p0 : p0 + piece].rearrange("p t s -> p s t"),
-                        scalar1=1.0,
-                        scalar2=0.0,
-                        op0=mybir.AluOpType.mult,
-                        op1=mybir.AluOpType.add,
-                    )
+                share = pixels - TENSOR_PIXELS
+                nc.gpsimd.tensor_scalar(
+                    out=grouped[u][:, :share, :],
+                    in0=packed[c][:, :, :share].rearrange("p t s -> p s t"),
+                    scalar1=1.0,
+                    scalar2=0.0,
+                    op0=mybir.AluOpType.mult,
+                    op1=mybir.AluOpType.add,
+                )
 
         def turn(c):
             u, s0, pixels = CHUNKS[c]
@@ -242,11 +240,11 @@ def tile_spectralchannelmixing_t_e_kernel(tc, x, wc_words, wc_scales, out):
         load_weights()
         for c in range(len(CHUNKS)):
             load_packed(c)
-        sort_words(0)
-        sort_scales(0)
+        for i in range(BLOCKS):
+            sort_words(i)
+            sort_scales(i)
         regroup(0)
         regroup_rest(0)
-        sort_scales(1)
 
         quant_round = {c * M_TILES - QUANT_LEAD[c]: c for c in range(len(CHUNKS))}
 
@@ -260,8 +258,6 @@ def tile_spectralchannelmixing_t_e_kernel(tc, x, wc_words, wc_scales, out):
                 gelu_and_store(k - GELU_LAG)
             if valid(k - ADD_LAG):
                 add_residual(k - ADD_LAG)
-            if k == SORT_ROUND:
-                sort_words(1)
             if valid(k) and STEPS[k][1] == 0 and STEPS[k][0] + 1 < len(CHUNKS):
                 regroup_rest(STEPS[k][0] + 1)
             if k in quant_round:

@@ -26,7 +26,9 @@ BANK_PIXELS = 256
 ADD_LAG = 1
 GELU_LAG = 3
 RESULT_UNITS = 6
+LAST_PIECE = 256
 STORE_ROWS = 2
+PAIRED_UNITS = 3
 
 CHUNKS = [(0, half * N_TILE, N_TILE) for half in range(HALVES)] + [
     (u, 0, PIXELS) for u in range(1, UNITS)
@@ -200,11 +202,13 @@ def tile_spectralchannelmixing_t_e_kernel(tc, x, wc_words, wc_scales, out):
             u, s0, pixels = CHUNKS[c]
             if t == 0 and s0 == 0:
                 result[u] = results.tile([P, M_TILES, PIXELS], F32, name="result")
-            for h0 in range(s0, s0 + pixels, N_TILE):
+            width = LAST_PIECE if k == len(STEPS) - 1 else N_TILE
+            for a0 in range(s0, s0 + pixels, width):
+                h0 = a0 - a0 % N_TILE
                 nc.vector.tensor_tensor(
-                    out=result[u][:, t, h0 : h0 + N_TILE],
-                    in0=acc[k, h0][:],
-                    in1=packed[c][:, t, h0 - s0 : h0 - s0 + N_TILE],
+                    out=result[u][:, t, a0 : a0 + width],
+                    in0=acc[k, h0][:, a0 - h0 : a0 - h0 + width],
+                    in1=packed[c][:, t, a0 - s0 : a0 - s0 + width],
                     op=mybir.AluOpType.add,
                 )
 
@@ -221,7 +225,7 @@ def tile_spectralchannelmixing_t_e_kernel(tc, x, wc_words, wc_scales, out):
             c, t = STEPS[k]
             u, s0, pixels = CHUNKS[c]
             last = k == len(STEPS) - 1
-            width = N_TILE if last else pixels
+            width = LAST_PIECE if last else N_TILE if u == UNITS - 1 else pixels
             for g0 in range(s0, s0 + pixels, width):
                 nc.scalar.activation(
                     out=result[u][:, t, g0 : g0 + width],
@@ -230,7 +234,7 @@ def tile_spectralchannelmixing_t_e_kernel(tc, x, wc_words, wc_scales, out):
                 )
                 if last:
                     store(u, t, 1, g0, width)
-            rows = 1 if u == UNITS - 1 else STORE_ROWS
+            rows = STORE_ROWS if u < PAIRED_UNITS else 1
             if not last and s0 + pixels == PIXELS and (t + 1) % rows == 0:
                 store(u, t + 1 - rows, rows, 0, PIXELS)
 

@@ -19,8 +19,10 @@ UNITS = BATCH * BLOCKS
 M_TILES = CD // P
 N_TILE = 512
 HALVES = PIXELS // N_TILE
-FIRST_SCALAR_PIXELS = (128, 128)
-TENSOR_PIXELS = 384
+SHARES = [
+    {"vector": 320, "scalar": 192},
+    {"vector": 256, "scalar": 256},
+] + [{"gpsimd": 512, "tensor": 512}] * 2 + [{"gpsimd": 640, "tensor": 384}] * 5
 TURN_PIXELS = P
 BANK_PIXELS = 256
 ADD_LAG = 1
@@ -34,7 +36,7 @@ CHUNKS = [(0, half * N_TILE, N_TILE) for half in range(HALVES)] + [
     (u, 0, PIXELS) for u in range(1, UNITS)
 ]
 STEPS = [(c, t) for c in range(len(CHUNKS)) for t in range(M_TILES)]
-QUANT_LEAD = [3, 3, 1] + [2] * (UNITS - 2)
+QUANT_LEAD = 2
 
 FLOPS = 2 * BATCH * PIXELS * BLOCKS * CD * CD
 
@@ -68,11 +70,13 @@ def tile_spectralchannelmixing_t_e_kernel(tc, x, wc_words, wc_scales, out):
         w_words = consts.tile([P, BLOCKS, 2 * CD], U8, align_bytes=64)
         w_scales = consts.tile([P, BLOCKS, CD], U8, align_bytes=64)
 
-        def load_weights():
+        def load_words():
             nc.sync.dma_start(
                 out=raw_words[:].bitcast(I32),
                 in_=wc_words.rearrange("g p n -> p g n").bitcast(I32),
             )
+
+        def load_scales():
             for quad in range(4):
                 nc.sync.dma_start(
                     out=raw_scales[32 * quad : 32 * quad + 4, :, :].bitcast(I32),
@@ -113,23 +117,23 @@ def tile_spectralchannelmixing_t_e_kernel(tc, x, wc_words, wc_scales, out):
                 ),
             )
 
+        def interleave(copy, c, first, last):
+            u, s0, pixels = CHUNKS[c]
+            copy(
+                out=grouped[u][:, s0 + first : s0 + last, :].rearrange("p (c r) t -> p c t r", r=4),
+                in_=packed[c][:, :, first:last].rearrange("p t (c r) -> p c t r", r=4),
+            )
+
         def regroup(c):
             u, s0, pixels = CHUNKS[c]
             if s0 == 0:
                 grouped[u] = regrouped.tile([P, PIXELS, PACK], BF16, align_bytes=64, name="grouped")
-            if u == 0:
-                share = pixels - FIRST_SCALAR_PIXELS[c]
-                if share > 0:
-                    nc.vector.tensor_copy(
-                        out=grouped[u][:, s0 : s0 + share, :].rearrange(
-                            "p (c r) t -> p c t r", r=4
-                        ),
-                        in_=packed[c][:, :, :share].rearrange("p t (c r) -> p c t r", r=4),
-                    )
-            else:
-                share = pixels - TENSOR_PIXELS
+            if "vector" in SHARES[c]:
+                interleave(nc.vector.tensor_copy, c, 0, SHARES[c]["vector"])
+            if "gpsimd" in SHARES[c]:
+                share = SHARES[c]["gpsimd"]
                 nc.gpsimd.tensor_scalar(
-                    out=grouped[u][:, :share, :],
+                    out=grouped[u][:, s0 : s0 + share, :],
                     in0=packed[c][:, :, :share].rearrange("p t s -> p s t"),
                     scalar1=1.0,
                     scalar2=0.0,
@@ -139,8 +143,9 @@ def tile_spectralchannelmixing_t_e_kernel(tc, x, wc_words, wc_scales, out):
 
         def turn(c):
             u, s0, pixels = CHUNKS[c]
-            for p0 in range(pixels - TENSOR_PIXELS, pixels, TURN_PIXELS):
-                bank, place = divmod(p0 - (pixels - TENSOR_PIXELS), BANK_PIXELS)
+            first = pixels - SHARES[c]["tensor"]
+            for p0 in range(first, pixels, TURN_PIXELS):
+                bank, place = divmod(p0 - first, BANK_PIXELS)
                 if place == 0:
                     turned[c, bank] = psum_turn.tile([P, BANK_PIXELS * PACK], BF16, name="turned")
                 nc.tensor.matmul(
@@ -153,21 +158,15 @@ def tile_spectralchannelmixing_t_e_kernel(tc, x, wc_words, wc_scales, out):
 
         def regroup_rest(c):
             u, s0, pixels = CHUNKS[c]
-            if u == 0:
-                r0 = pixels - FIRST_SCALAR_PIXELS[c]
-                nc.scalar.copy(
-                    out=grouped[u][:, s0 + r0 : s0 + pixels, :].rearrange(
-                        "p (c r) t -> p c t r", r=4
-                    ),
-                    in_=packed[c][:, :, r0:].rearrange("p t (c r) -> p c t r", r=4),
-                )
+            if "scalar" in SHARES[c]:
+                interleave(nc.scalar.copy, c, pixels - SHARES[c]["scalar"], pixels)
             else:
-                for p0 in range(pixels - TENSOR_PIXELS, pixels, BANK_PIXELS):
+                first = pixels - SHARES[c]["tensor"]
+                for p0 in range(first, pixels, BANK_PIXELS):
                     width = min(BANK_PIXELS, pixels - p0)
-                    bank = (p0 - (pixels - TENSOR_PIXELS)) // BANK_PIXELS
                     nc.scalar.copy(
                         out=grouped[u][:, p0 : p0 + width, :].rearrange("p s t -> p (s t)"),
-                        in_=turned[c, bank][:, : width * PACK],
+                        in_=turned[c, (p0 - first) // BANK_PIXELS][:, : width * PACK],
                     )
 
         def quantise(c):
@@ -241,18 +240,23 @@ def tile_spectralchannelmixing_t_e_kernel(tc, x, wc_words, wc_scales, out):
         def valid(k):
             return 0 <= k < len(STEPS)
 
-        load_weights()
-        for c in range(len(CHUNKS)):
+        load_words()
+        load_packed(0)
+        load_scales()
+        for c in range(1, len(CHUNKS)):
             load_packed(c)
         for i in range(BLOCKS):
             sort_words(i)
-            sort_scales(i)
-        regroup(0)
-        regroup_rest(0)
+        for c in range(HALVES):
+            regroup(c)
+            regroup_rest(c)
+            quantise(c)
+            sort_scales(c)
+        regroup(HALVES)
 
-        quant_round = {c * M_TILES - QUANT_LEAD[c]: c for c in range(len(CHUNKS))}
+        quant_round = {c * M_TILES - QUANT_LEAD: c for c in range(HALVES, len(CHUNKS))}
 
-        for k in range(-QUANT_LEAD[0], len(STEPS) + GELU_LAG):
+        for k in range(len(STEPS) + GELU_LAG):
             if valid(k):
                 multiply(k)
             if valid(k + 1) and STEPS[k + 1][1] == 0 and STEPS[k + 1][0] + 1 < len(CHUNKS):
@@ -262,7 +266,7 @@ def tile_spectralchannelmixing_t_e_kernel(tc, x, wc_words, wc_scales, out):
                 gelu_and_store(k - GELU_LAG)
             if valid(k - ADD_LAG):
                 add_residual(k - ADD_LAG)
-            if valid(k) and STEPS[k][1] == 0 and STEPS[k][0] + 1 < len(CHUNKS):
+            if valid(k) and STEPS[k][1] == 0 and HALVES <= STEPS[k][0] + 1 < len(CHUNKS):
                 regroup_rest(STEPS[k][0] + 1)
             if k in quant_round:
                 quantise(quant_round[k])

@@ -22,7 +22,8 @@ HALVES = PIXELS // N_TILE
 SHARES = [
     {"vector": 320, "scalar": 192},
     {"vector": 256, "scalar": 256},
-] + [{"gpsimd": 512, "tensor": 512}] * 2 + [{"gpsimd": 640, "tensor": 384}] * 5
+    {"gpsimd": 448, "scalar": 576},
+] + [{"gpsimd": 512, "tensor": 512}] * 2 + [{"gpsimd": 640, "tensor": 384}] * 4
 TURN_PIXELS = P
 BANK_PIXELS = 256
 ADD_LAG = 1
@@ -247,12 +248,16 @@ def tile_spectralchannelmixing_t_e_kernel(tc, x, wc_words, wc_scales, out):
             load_packed(c)
         for i in range(BLOCKS):
             sort_words(i)
-        for c in range(HALVES):
-            regroup(c)
-            regroup_rest(c)
-            quantise(c)
-            sort_scales(c)
-        regroup(HALVES)
+        regroup(0)
+        regroup_rest(0)
+        quantise(0)
+        regroup(1)
+        regroup_rest(1)
+        sort_scales(0)
+        quantise(1)
+        regroup(2)
+        regroup_rest(2)
+        sort_scales(1)
 
         quant_round = {c * M_TILES - QUANT_LEAD: c for c in range(HALVES, len(CHUNKS))}
 
@@ -260,14 +265,15 @@ def tile_spectralchannelmixing_t_e_kernel(tc, x, wc_words, wc_scales, out):
             if valid(k):
                 multiply(k)
             if valid(k + 1) and STEPS[k + 1][1] == 0 and STEPS[k + 1][0] + 1 < len(CHUNKS):
-                if CHUNKS[STEPS[k + 1][0] + 1][0] > 0:
+                if "tensor" in SHARES[STEPS[k + 1][0] + 1]:
                     turn(STEPS[k + 1][0] + 1)
             if valid(k - GELU_LAG):
                 gelu_and_store(k - GELU_LAG)
             if valid(k - ADD_LAG):
                 add_residual(k - ADD_LAG)
-            if valid(k) and STEPS[k][1] == 0 and HALVES <= STEPS[k][0] + 1 < len(CHUNKS):
-                regroup_rest(STEPS[k][0] + 1)
+            if valid(k) and STEPS[k][1] == 0 and STEPS[k][0] + 1 < len(CHUNKS):
+                if "tensor" in SHARES[STEPS[k][0] + 1]:
+                    regroup_rest(STEPS[k][0] + 1)
             if k in quant_round:
                 quantise(quant_round[k])
                 if quant_round[k] + 1 < len(CHUNKS):

@@ -29,6 +29,7 @@ BANK_PIXELS = 256
 ADD_LAG = 1
 GELU_LAG = 3
 RESULT_UNITS = 6
+FINE_UNITS = (UNITS - 2, UNITS - 1)
 LAST_PIECE = 256
 STORE_ROWS = 2
 PAIRED_UNITS = 3
@@ -36,6 +37,7 @@ PAIRED_UNITS = 3
 CHUNKS = [(0, half * N_TILE, N_TILE) for half in range(HALVES)] + [
     (u, 0, PIXELS) for u in range(1, UNITS)
 ]
+LOADS = [(0,), (1,), (2,), (3,), (4, 5), (6, 7), (8,)]
 STEPS = [(c, t) for c in range(len(CHUNKS)) for t in range(M_TILES)]
 QUANT_LEAD = 2
 
@@ -44,13 +46,12 @@ FLOPS = 2 * BATCH * PIXELS * BLOCKS * CD * CD
 
 def tile_spectralchannelmixing_t_e_kernel(tc, x, wc_words, wc_scales, out):
     nc = tc.nc
-    x_rows = x.rearrange("b c h w -> b c (h w)")
+    x_rows = x.rearrange("b c h w -> (b c) (h w)")
     out_rows = out.rearrange("b c h w -> b c (h w)")
 
     with (
         tc.tile_pool(name="consts", bufs=1) as consts,
-        tc.tile_pool(name="inputs", bufs=UNITS - 1) as inputs,
-        tc.tile_pool(name="first_inputs", bufs=HALVES) as first_inputs,
+        tc.tile_pool(name="inputs", bufs=1) as inputs,
         tc.tile_pool(name="regrouped", bufs=1) as regrouped,
         tc.tile_pool(name="quant", bufs=UNITS) as quant,
         tc.tile_pool(name="results", bufs=RESULT_UNITS) as results,
@@ -106,17 +107,18 @@ def tile_spectralchannelmixing_t_e_kernel(tc, x, wc_words, wc_scales, out):
         acc = {}
         result = {}
 
-        def load_packed(c):
-            u, s0, pixels = CHUNKS[c]
-            b, i = divmod(u, BLOCKS)
-            pool = inputs if pixels == PIXELS else first_inputs
-            packed[c] = pool.tile([P, PACK, pixels], BF16, name="packed")
+        def load_packed(chunks):
+            u, s0, pixels = CHUNKS[chunks[0]]
+            count = len(chunks)
+            tile = inputs.tile([P, count, PACK, pixels], BF16, name="packed%d" % chunks[0])
             nc.sync.dma_start(
-                out=packed[c][:],
-                in_=x_rows[b, i * CD : (i + 1) * CD, s0 : s0 + pixels].rearrange(
-                    "(p t) s -> p t s", t=PACK
+                out=tile[:],
+                in_=x_rows[u * CD : (u + count) * CD, s0 : s0 + pixels].rearrange(
+                    "(i p t) s -> p i t s", i=count, t=PACK
                 ),
             )
+            for j, c in enumerate(chunks):
+                packed[c] = tile[:, j]
 
         def interleave(copy, c, first, last):
             u, s0, pixels = CHUNKS[c]
@@ -225,7 +227,7 @@ def tile_spectralchannelmixing_t_e_kernel(tc, x, wc_words, wc_scales, out):
             c, t = STEPS[k]
             u, s0, pixels = CHUNKS[c]
             last = k == len(STEPS) - 1
-            width = LAST_PIECE if last else N_TILE if u == UNITS - 1 else pixels
+            width = LAST_PIECE if last else N_TILE if u in FINE_UNITS else pixels
             for g0 in range(s0, s0 + pixels, width):
                 nc.scalar.activation(
                     out=result[u][:, t, g0 : g0 + width],
@@ -242,10 +244,10 @@ def tile_spectralchannelmixing_t_e_kernel(tc, x, wc_words, wc_scales, out):
             return 0 <= k < len(STEPS)
 
         load_words()
-        load_packed(0)
+        load_packed(LOADS[0])
         load_scales()
-        for c in range(1, len(CHUNKS)):
-            load_packed(c)
+        for chunks in LOADS[1:]:
+            load_packed(chunks)
         for i in range(BLOCKS):
             sort_words(i)
         regroup(0)

@@ -22,13 +22,14 @@ HALVES = PIXELS // N_TILE
 SHARES = [
     {"vector": 320, "scalar": 192},
     {"vector": 256, "scalar": 256},
-    {"gpsimd": 448, "scalar": 576},
-] + [{"gpsimd": 512, "tensor": 512}] * 2 + [{"gpsimd": 640, "tensor": 384}] * 4
+    {"gpsimd": 512, "scalar": 512},
+    {"gpsimd": 512, "tensor": 512},
+] + [{"gpsimd": 640, "tensor": 384}] * 5
 TURN_PIXELS = P
 BANK_PIXELS = 256
 ADD_LAG = 1
 GELU_LAG = 3
-RESULT_UNITS = 6
+CODE_UNITS = 3
 FINE_UNITS = (UNITS - 2, UNITS - 1)
 LAST_PIECE = 256
 STORE_ROWS = 2
@@ -53,8 +54,8 @@ def tile_spectralchannelmixing_t_e_kernel(tc, x, wc_words, wc_scales, out):
         tc.tile_pool(name="consts", bufs=1) as consts,
         tc.tile_pool(name="inputs", bufs=1) as inputs,
         tc.tile_pool(name="regrouped", bufs=1) as regrouped,
-        tc.tile_pool(name="quant", bufs=UNITS) as quant,
-        tc.tile_pool(name="results", bufs=RESULT_UNITS) as results,
+        tc.tile_pool(name="quant", bufs=CODE_UNITS) as quant,
+        tc.tile_pool(name="results", bufs=UNITS) as results,
         tc.psum_pool(name="psum_mix", bufs=3 * HALVES) as psum_mix,
         tc.psum_pool(name="psum_turn", bufs=2) as psum_turn,
         tc.manual_schedule(),

@@ -32,13 +32,12 @@ GELU_LAG = 3
 CODE_UNITS = 3
 FINE_UNITS = (UNITS - 2, UNITS - 1)
 LAST_PIECE = 256
-STORE_ROWS = 2
-PAIRED_UNITS = 3
+STORE_ROWS = [4] * 3 + [2] * 3 + [1] * 2
 
 CHUNKS = [(0, half * N_TILE, N_TILE) for half in range(HALVES)] + [
     (u, 0, PIXELS) for u in range(1, UNITS)
 ]
-LOADS = [(0,), (1,), (2,), (3,), (4, 5), (6, 7), (8,)]
+LOADS = [(0,), (1,), (2,), (3,), (4, 5), (6, 7, 8)]
 STEPS = [(c, t) for c in range(len(CHUNKS)) for t in range(M_TILES)]
 QUANT_LEAD = 2
 
@@ -237,7 +236,7 @@ def tile_spectralchannelmixing_t_e_kernel(tc, x, wc_words, wc_scales, out):
                 )
                 if last:
                     store(u, t, 1, g0, width)
-            rows = STORE_ROWS if u < PAIRED_UNITS else 1
+            rows = STORE_ROWS[u]
             if not last and s0 + pixels == PIXELS and (t + 1) % rows == 0:
                 store(u, t + 1 - rows, rows, 0, PIXELS)
 

import concourse.mybir as mybir
from concourse.masks import make_identity

BF16 = mybir.dt.bfloat16
F32 = mybir.dt.float32
I32 = mybir.dt.int32
U8 = mybir.dt.uint8
U32 = mybir.dt.uint32
FP8X4 = mybir.dt.float8_e4m3fn_x4
FP4X4 = mybir.dt.float4_e2m1fn_x4

P = 128
PACK = 4
BATCH = 4
BLOCKS = 2
CD = P * PACK
PIXELS = 32 * 32
UNITS = BATCH * BLOCKS
M_TILES = CD // P
N_TILE = 512
HALVES = PIXELS // N_TILE
SHARES = [
    {"vector": 320, "scalar": 192},
    {"vector": 256, "scalar": 256},
    {"gpsimd": 512, "scalar": 512},
    {"gpsimd": 512, "tensor": 512},
] + [{"gpsimd": 640, "tensor": 384}] * 5
TURN_PIXELS = P
BANK_PIXELS = 256
ADD_LAG = 1
GELU_LAG = 3
CODE_UNITS = 3
FINE_UNITS = (UNITS - 2, UNITS - 1)
LAST_PIECE = 256
STORE_ROWS = [4] * 3 + [2] * 3 + [1] * 2

CHUNKS = [(0, half * N_TILE, N_TILE) for half in range(HALVES)] + [
    (u, 0, PIXELS) for u in range(1, UNITS)
]
LOADS = [(0,), (1,), (2,), (3,), (4, 5), (6, 7, 8)]
STEPS = [(c, t) for c in range(len(CHUNKS)) for t in range(M_TILES)]
QUANT_LEAD = 2

FLOPS = 2 * BATCH * PIXELS * BLOCKS * CD * CD


def tile_spectralchannelmixing_t_e_kernel(tc, x, wc_words, wc_scales, out):
    nc = tc.nc
    x_rows = x.rearrange("b c h w -> (b c) (h w)")
    out_rows = out.rearrange("b c h w -> b c (h w)")

    with (
        tc.tile_pool(name="consts", bufs=1) as consts,
        tc.tile_pool(name="inputs", bufs=1) as inputs,
        tc.tile_pool(name="regrouped", bufs=1) as regrouped,
        tc.tile_pool(name="quant", bufs=CODE_UNITS) as quant,
        tc.tile_pool(name="results", bufs=UNITS) as results,
        tc.psum_pool(name="psum_mix", bufs=3 * HALVES) as psum_mix,
        tc.psum_pool(name="psum_turn", bufs=2) as psum_turn,
        tc.manual_schedule(),
    ):
        warm = consts.tile([P, 1], F32)
        nc.vector.memset(warm[:], 0.0)
        nc.scalar.activation(out=warm[:], in_=warm[:], func=mybir.ActivationFunctionType.Gelu)

        identity = consts.tile([P, P], BF16)
        make_identity(nc, identity[:])

        raw_words = consts.tile([P, BLOCKS, 2 * CD], U8)
        raw_scales = consts.tile([P, BLOCKS, CD], U8)
        nc.vector.memset(raw_scales[:].bitcast(I32), 0)
        w_words = consts.tile([P, BLOCKS, 2 * CD], U8, align_bytes=64)
        w_scales = consts.tile([P, BLOCKS, CD], U8, align_bytes=64)

        def load_words():
            nc.sync.dma_start(
                out=raw_words[:].bitcast(I32),
                in_=wc_words.rearrange("g p n -> p g n").bitcast(I32),
            )

        def load_scales():
            for quad in range(4):
                nc.sync.dma_start(
                    out=raw_scales[32 * quad : 32 * quad + 4, :, :].bitcast(I32),
                    in_=wc_scales[:, 4 * quad : 4 * quad + 4, :]
                    .rearrange("g r n -> r g n")
                    .bitcast(I32),
                )

        def sort_words(i):
            nc.vector.tensor_copy(
                out=w_words[:, i, :].rearrange("p (t q b) -> p t q b", t=M_TILES, b=2),
                in_=raw_words[:, i, :].rearrange("p (q t b) -> p t q b", t=M_TILES, b=2),
            )

        def sort_scales(i):
            nc.vector.tensor_copy(
                out=w_scales[:, i, :].rearrange("p (t q) -> p t q", t=M_TILES),
                in_=raw_scales[:, i, :].rearrange("p (q t) -> p t q", t=M_TILES),
            )

        packed = {}
        grouped = {}
        turned = {}
        x_codes = {}
        x_scales = {}
        acc = {}
        result = {}

        def load_packed(chunks):
            u, s0, pixels = CHUNKS[chunks[0]]
            count = len(chunks)
            tile = inputs.tile([P, count, PACK, pixels], BF16, name="packed%d" % chunks[0])
            nc.sync.dma_start(
                out=tile[:],
                in_=x_rows[u * CD : (u + count) * CD, s0 : s0 + pixels].rearrange(
                    "(i p t) s -> p i t s", i=count, t=PACK
                ),
            )
            for j, c in enumerate(chunks):
                packed[c] = tile[:, j]

        def interleave(copy, c, first, last):
            u, s0, pixels = CHUNKS[c]
            copy(
                out=grouped[u][:, s0 + first : s0 + last, :].rearrange("p (c r) t -> p c t r", r=4),
                in_=packed[c][:, :, first:last].rearrange("p t (c r) -> p c t r", r=4),
            )

        def regroup(c):
            u, s0, pixels = CHUNKS[c]
            if s0 == 0:
                grouped[u] = regrouped.tile([P, PIXELS, PACK], BF16, align_bytes=64, name="grouped")
            if "vector" in SHARES[c]:
                interleave(nc.vector.tensor_copy, c, 0, SHARES[c]["vector"])
            if "gpsimd" in SHARES[c]:
                share = SHARES[c]["gpsimd"]
                nc.gpsimd.tensor_scalar(
                    out=grouped[u][:, s0 : s0 + share, :],
                    in0=packed[c][:, :, :share].rearrange("p t s -> p s t"),
                    scalar1=1.0,
                    scalar2=0.0,
                    op0=mybir.AluOpType.mult,
                    op1=mybir.AluOpType.add,
                )

        def turn(c):
            u, s0, pixels = CHUNKS[c]
            first = pixels - SHARES[c]["tensor"]
            for p0 in range(first, pixels, TURN_PIXELS):
                bank, place = divmod(p0 - first, BANK_PIXELS)
                if place == 0:
                    turned[c, bank] = psum_turn.tile([P, BANK_PIXELS * PACK], BF16, name="turned")
                nc.tensor.matmul(
                    out=turned[c, bank][:, place * PACK : (place + TURN_PIXELS) * PACK],
                    lhsT=identity[:],
                    rhs=packed[c][:, :, p0 : p0 + TURN_PIXELS].rearrange("p t s -> p s t"),
                    start=True,
                    stop=True,
                )

        def regroup_rest(c):
            u, s0, pixels = CHUNKS[c]
            if "scalar" in SHARES[c]:
                interleave(nc.scalar.copy, c, pixels - SHARES[c]["scalar"], pixels)
            else:
                first = pixels - SHARES[c]["tensor"]
                for p0 in range(first, pixels, BANK_PIXELS):
                    width = min(BANK_PIXELS, pixels - p0)
                    nc.scalar.copy(
                        out=grouped[u][:, p0 : p0 + width, :].rearrange("p s t -> p (s t)"),
                        in_=turned[c, (p0 - first) // BANK_PIXELS][:, : width * PACK],
                    )

        def quantise(c):
            u, s0, pixels = CHUNKS[c]
            if s0 == 0:
                x_codes[u] = quant.tile([P, PIXELS], U32, align_bytes=64, name="x_codes")
                x_scales[u] = quant.tile([P, PIXELS], U8, align_bytes=64, name="x_scales")
            nc.vector.quantize_mx(
                out=x_codes[u][:, s0 : s0 + pixels].bitcast(FP8X4),
                scales=x_scales[u][:, s0 : s0 + pixels],
                in_=grouped[u][:, s0 : s0 + pixels, :].rearrange("p s t -> p (s t)"),
            )

        def multiply(k):
            c, t = STEPS[k]
            u, s0, pixels = CHUNKS[c]
            i = u % BLOCKS
            for h0 in range(s0, s0 + pixels, N_TILE):
                acc[k, h0] = psum_mix.tile([P, N_TILE], F32, name="acc")
                nc.tensor.matmul_mx(
                    out=acc[k, h0][:],
                    lhsT=w_words[:, i, 2 * P * t : 2 * P * (t + 1)].bitcast(FP4X4),
                    lhsT_scale=w_scales[:, i, P * t : P * (t + 1)],
                    rhs=x_codes[u][:, h0 : h0 + N_TILE].bitcast(FP8X4),
                    rhs_scale=x_scales[u][:, h0 : h0 + N_TILE],
                    start=True,
                    stop=True,
                )

        def add_residual(k):
            c, t = STEPS[k]
            u, s0, pixels = CHUNKS[c]
            if t == 0 and s0 == 0:
                result[u] = results.tile([P, M_TILES, PIXELS], F32, name="result")
            width = LAST_PIECE if k == len(STEPS) - 1 else N_TILE
            for a0 in range(s0, s0 + pixels, width):
                h0 = a0 - a0 % N_TILE
                nc.vector.tensor_tensor(
                    out=result[u][:, t, a0 : a0 + width],
                    in0=acc[k, h0][:, a0 - h0 : a0 - h0 + width],
                    in1=packed[c][:, t, a0 - s0 : a0 - s0 + width],
                    op=mybir.AluOpType.add,
                )

        def store(u, t, rows, s0, pixels):
            b, i = divmod(u, BLOCKS)
            nc.sync.dma_start(
                out=out_rows[b, i * CD : (i + 1) * CD, s0 : s0 + pixels].rearrange(
                    "(q t) s -> q t s", t=M_TILES
                )[:, t : t + rows, :],
                in_=result[u][:, t : t + rows, s0 : s0 + pixels],
            )

        def gelu_and_store(k):
            c, t = STEPS[k]
            u, s0, pixels = CHUNKS[c]
            last = k == len(STEPS) - 1
            width = LAST_PIECE if last else N_TILE if u in FINE_UNITS else pixels
            for g0 in range(s0, s0 + pixels, width):
                nc.scalar.activation(
                    out=result[u][:, t, g0 : g0 + width],
                    in_=result[u][:, t, g0 : g0 + width],
                    func=mybir.ActivationFunctionType.Gelu,
                )
                if last:
                    store(u, t, 1, g0, width)
            rows = STORE_ROWS[u]
            if not last and s0 + pixels == PIXELS and (t + 1) % rows == 0:
                store(u, t + 1 - rows, rows, 0, PIXELS)

        def valid(k):
            return 0 <= k < len(STEPS)

        load_words()
        load_packed(LOADS[0])
        load_scales()
        for chunks in LOADS[1:]:
            load_packed(chunks)
        for i in range(BLOCKS):
            sort_words(i)
        regroup(0)
        regroup_rest(0)
        quantise(0)
        regroup(1)
        regroup_rest(1)
        sort_scales(0)
        quantise(1)
        regroup(2)
        regroup_rest(2)
        sort_scales(1)

        quant_round = {c * M_TILES - QUANT_LEAD: c for c in range(HALVES, len(CHUNKS))}

        for k in range(len(STEPS) + GELU_LAG):
            if valid(k):
                multiply(k)
            if valid(k + 1) and STEPS[k + 1][1] == 0 and STEPS[k + 1][0] + 1 < len(CHUNKS):
                if "tensor" in SHARES[STEPS[k + 1][0] + 1]:
                    turn(STEPS[k + 1][0] + 1)
            if valid(k - GELU_LAG):
                gelu_and_store(k - GELU_LAG)
            if valid(k - ADD_LAG):
                add_residual(k - ADD_LAG)
            if valid(k) and STEPS[k][1] == 0 and STEPS[k][0] + 1 < len(CHUNKS):
                if "tensor" in SHARES[STEPS[k][0] + 1]:
                    regroup_rest(STEPS[k][0] + 1)
            if k in quant_round:
                quantise(quant_round[k])
                if quant_round[k] + 1 < len(CHUNKS):
                    regroup(quant_round[k] + 1)
